import numpy as np
import ml_dtypes


def mxq(x, axis, fmt="e4m3"):
    dtype, down = {"e4m3": (ml_dtypes.float8_e4m3fn, 7), "e5m2": (ml_dtypes.float8_e5m2, 14)}[fmt]
    v = np.moveaxis(np.asarray(x, np.float32).astype(ml_dtypes.bfloat16).astype(np.float64), axis, -1)
    blocks = v.reshape(v.shape[:-1] + (-1, 32))
    amax = np.abs(blocks).max(-1, keepdims=True)
    byte = np.maximum(np.where(amax > 0, np.frexp(amax)[1] - 1 + 127, 0) - down, 1)
    scale = np.exp2(byte - 127.0)
    codes = (blocks / scale).astype(np.float32).astype(dtype).astype(np.float64)
    return np.moveaxis((codes * scale).reshape(v.shape), -1, axis)


WIDE = False


def mx_kscale(k):
    if not WIDE:
        return np.ones(k)
    levels = np.array([10, -10, 5, -5, 0])
    a = np.random.permutation(np.resize(levels, k // 512 * 4)).reshape(k // 512, 4)
    idx = np.arange(k)
    return np.exp2(a[idx // 512, idx % 128 // 32])


BF16 = ml_dtypes.bfloat16


def bf(x):
    return np.asarray(x, np.float32).astype(BF16)


def f64(x):
    return np.asarray(x).astype(np.float64)


E2M1 = np.array([0.0, 0.5, 1.0, 1.5, 2.0, 3.0, 4.0, 6.0, -0.0, -0.5, -1.0, -1.5, -2.0, -3.0, -4.0, -6.0])


def pack_weight(w, fmt):
    k, n = w.shape
    w = f64(bf(w)).reshape(k // 32, 32, n)
    amax = np.abs(w).max(1)
    if fmt == "e4m3":
        byte = np.frexp(amax)[1] - 1 + 127 - 7
    else:
        mant, ex = np.frexp(amax / 6.0)
        byte = np.where(mant > 0.5, ex, ex - 1) + 127
    byte = np.clip(np.where(amax > 0, byte, 1), 1, 254)
    scaled = (w * np.exp2(127.0 - byte)[:, None, :]).reshape(k, n).astype(np.float32)
    by_word = np.ascontiguousarray(scaled.reshape(k // 512, 128, 4, n).transpose(0, 1, 3, 2))
    if fmt == "e4m3":
        words = by_word.astype(ml_dtypes.float8_e4m3fn).view(np.uint8)
    else:
        c = by_word.astype(ml_dtypes.float4_e2m1fn).view(np.uint8) & 0xF
        words = c[..., 0::2] | (c[..., 1::2] << 4)
    return np.ascontiguousarray(words), np.ascontiguousarray(byte.astype(np.uint8).reshape(k // 512, 16, n))


def unpack_weight(words, scales, fmt):
    g, p, n, _ = words.shape
    if fmt == "e4m3":
        vals = np.ascontiguousarray(words).view(ml_dtypes.float8_e4m3fn).astype(np.float64)
    else:
        nib = np.empty((g, p, n, 4), np.uint8)
        nib[..., 0::2] = words & 0xF
        nib[..., 1::2] = words >> 4
        vals = E2M1[nib]
    vals = vals * np.repeat(np.exp2(scales.astype(np.float64) - 127.0), 8, axis=1)[..., None]
    return vals.transpose(0, 1, 3, 2).reshape(g * 512, n)


B, S, D, H, KV, DH, QB = 1, 1024, 1024, 16, 4, 128, 512
HALF = DH // 2
EPS = 1e-6
FMT = "e4m3"


def rope_tables():
    inv_freq = 1.0 / (10000.0 ** (np.arange(HALF) / HALF))
    ang = np.arange(S)[:, None] * inv_freq[None, :]
    ang = np.concatenate([ang, ang], axis=-1)
    return np.sin(ang), np.cos(ang)


def rmsnorm(u, scale, shift):
    rms = np.sqrt(np.mean(u * u, axis=-1, keepdims=True) + EPS)
    return u / rms * (1.0 + scale) + shift


def apply_rope(u, sin, cos):
    rot = np.concatenate([-u[..., HALF:], u[..., :HALF]], axis=-1)
    return u * cos[None, None, :S, :] + rot * sin[None, None, :S, :]


def heads(u, n):
    return u.reshape(B, S, n, DH).transpose(0, 2, 1, 3)


def setup_inputs():
    s = mx_kscale(D)
    sin, cos = rope_tables()
    x = bf(np.random.standard_normal((B, S, D)) * s)
    wq_words, wq_scales = pack_weight(np.ascontiguousarray((np.random.standard_normal((H * DH, D)) / np.sqrt(D) / s).T), FMT)
    wk_words, wk_scales = pack_weight(np.ascontiguousarray((np.random.standard_normal((KV * DH, D)) / np.sqrt(D) / s).T), FMT)
    wv_words, wv_scales = pack_weight(np.ascontiguousarray((np.random.standard_normal((KV * DH, D)) * 2.0 / np.sqrt(D) / s).T), FMT)
    return {"x": x,
            "sin_thetas": bf(sin), "cos_thetas": bf(cos),
            "wq_words": wq_words, "wq_scales": wq_scales,
            "wk_words": wk_words, "wk_scales": wk_scales,
            "wv_words": wv_words, "wv_scales": wv_scales,
            "q_scale": bf(np.random.standard_normal(DH) * 0.1), "q_shift": bf(np.random.standard_normal(DH) * 0.1),
            "k_scale": bf(np.random.standard_normal(DH) * 0.1), "k_shift": bf(np.random.standard_normal(DH) * 0.1)}


def reference(x, sin_thetas, cos_thetas, wq_words, wq_scales, wk_words, wk_scales, wv_words, wv_scales, q_scale, q_shift, k_scale, k_shift):
    xq = mxq(f64(x), 2, "e4m3")
    q = heads(xq @ unpack_weight(wq_words, wq_scales, FMT), H)
    k = heads(xq @ unpack_weight(wk_words, wk_scales, FMT), KV)
    v = heads(xq @ unpack_weight(wv_words, wv_scales, FMT), KV)
    q = rmsnorm(q, f64(q_scale), f64(q_shift))
    k = rmsnorm(k, f64(k_scale), f64(k_shift))
    q = apply_rope(q, f64(sin_thetas), f64(cos_thetas))
    k = apply_rope(k, f64(sin_thetas), f64(cos_thetas))
    return q, k, v

@@ -1,0 +1,280 @@
+from contextlib import ExitStack
+
+import concourse.masks as masks
+import concourse.mybir as mybir
+
+F32 = mybir.dt.float32
+BF16 = mybir.dt.bfloat16
+U8 = mybir.dt.uint8
+U32 = mybir.dt.uint32
+I32 = mybir.dt.int32
+FP8X4 = mybir.dt.float8_e4m3fn_x4
+ACT = mybir.ActivationFunctionType
+ALU = mybir.AluOpType
+
+P = 128
+S = 1024
+D = 1024
+DH = 128
+HALF = DH // 2
+Q_HEADS = 16
+KV_HEADS = 4
+EPS = 1e-6
+
+PACK = 4
+K_PASS = P * PACK
+PASSES = D // K_PASS
+SLOTS = S // P
+N_TILE = 512
+TILE_HEADS = N_TILE // DH
+ROUND_SLOTS = 2
+ROUNDS = SLOTS // ROUND_SLOTS
+ROUND_HEADS = ROUND_SLOTS * TILE_HEADS
+
+Q_COLS = Q_HEADS * DH
+K_COL0 = Q_COLS
+V_COL0 = Q_COLS + KV_HEADS * DH
+N_ALL = Q_COLS + 2 * KV_HEADS * DH
+
+FLOPS = 2 * S * D * N_ALL
+
+
+def tile_groupqueryattention_pa_kernel(
+    tc,
+    x,
+    sin_thetas,
+    cos_thetas,
+    wq_words,
+    wq_scales,
+    wk_words,
+    wk_scales,
+    wv_words,
+    wv_scales,
+    q_scale,
+    q_shift,
+    k_scale,
+    k_shift,
+    out_0,
+    out_1,
+    out_2,
+):
+    nc = tc.nc
+    with ExitStack() as ctx:
+        keep = ctx.enter_context(tc.tile_pool(name="keep", bufs=1))
+        stats = ctx.enter_context(tc.tile_pool(name="stats", bufs=6))
+        work = ctx.enter_context(tc.tile_pool(name="work", bufs=3))
+        results = ctx.enter_context(tc.tile_pool(name="results", bufs=6))
+        psum_x = ctx.enter_context(tc.psum_pool(name="psum_x", bufs=2))
+        psum_acc = ctx.enter_context(tc.psum_pool(name="psum_acc", bufs=6))
+
+        w_planes = keep.tile([P, N_ALL], U8, align_bytes=64)
+        nc.vector.memset(w_planes[:].bitcast(I32), 0)
+        eps = keep.tile([P, 1], F32)
+        nc.vector.memset(eps[:], EPS)
+        identity = keep.tile([P, P], F32)
+        masks.make_identity(nc, identity[:])
+
+        vectors = keep.tile([P, 4, DH], BF16)
+        for i, vector in enumerate((q_scale, q_shift, k_scale, k_shift)):
+            nc.scalar.dma_start(out=vectors[:, i, :], in_=vector.partition_broadcast(P))
+        cos_sb = keep.tile([P, SLOTS, DH], BF16)
+        sin_sb = keep.tile([P, SLOTS, DH], BF16)
+        nc.scalar.dma_start(out=cos_sb[:], in_=cos_thetas.rearrange("(p j) d -> p j d", j=SLOTS))
+        nc.scalar.dma_start(out=sin_sb[:], in_=sin_thetas.rearrange("(p j) d -> p j d", j=SLOTS))
+        table_warm = keep.tile([P, 1], F32)
+        nc.scalar.activation(out=table_warm[:], in_=eps[:], func=ACT.Sqrt)
+
+        x_sb = keep.tile([P, SLOTS, D], BF16)
+        x_rows = x.flatten_outer_dims().rearrange("(p j) k -> p j k", j=SLOTS)
+        w_words = keep.tile([P, PASSES, N_ALL], U32, align_bytes=64)
+
+        def load_x(r):
+            slots = slice(r * ROUND_SLOTS, (r + 1) * ROUND_SLOTS)
+            nc.sync.dma_start(out=x_sb[:, slots, :], in_=x_rows[:, slots, :])
+
+        def load_scales(scales, col0):
+            width = scales.shape[2]
+            for quadrant in range(4):
+                nc.sync.dma_start(
+                    out=w_planes[32 * quadrant : 32 * quadrant + 4 * PASSES, col0 : col0 + width].bitcast(I32),
+                    in_=scales[:, 4 * quadrant : 4 * quadrant + 4, :].bitcast(I32),
+                )
+
+        def load_words(words, col0, first, width):
+            for g in range(PASSES):
+                nc.sync.dma_start(
+                    out=w_words[:, g, col0 + first : col0 + first + width].bitcast(I32),
+                    in_=words[g].rearrange("p n t -> p (n t)")[:, PACK * first : PACK * (first + width)].bitcast(I32),
+                )
+
+        load_x(0)
+        load_scales(wq_scales, 0)
+        load_words(wq_words, 0, 0, N_TILE)
+        for r in range(1, ROUNDS):
+            load_x(r)
+        load_scales(wv_scales, V_COL0)
+        load_words(wv_words, V_COL0, 0, N_TILE)
+        load_words(wq_words, 0, N_TILE, Q_COLS - N_TILE)
+        load_scales(wk_scales, K_COL0)
+        load_words(wk_words, K_COL0, 0, N_TILE)
+
+        def rotated(vector, name):
+            rot = keep.tile([P, DH], F32, name=name)
+            nc.vector.tensor_scalar_mul(out=rot[:, 0:HALF], in0=vector[:, HALF:DH], scalar1=-1.0)
+            nc.vector.tensor_copy(out=rot[:, HALF:DH], in_=vector[:, 0:HALF])
+            return rot
+
+        def over_slots(vector):
+            return vector.unsqueeze(1).to_broadcast([P, SLOTS, DH])
+
+        def rope_tables(scale, shift, ab_engine, which):
+            gain = keep.tile([P, DH], F32, name="gain_" + which)
+            nc.vector.tensor_scalar_add(out=gain[:], in0=scale, scalar1=1.0)
+            gain_rot = rotated(gain[:], "gain_rot_" + which)
+            shift_rot = rotated(shift, "shift_rot_" + which)
+            a = keep.tile([P, SLOTS, DH], F32, name="a_" + which)
+            b = keep.tile([P, SLOTS, DH], F32, name="b_" + which)
+            c = keep.tile([P, SLOTS, DH], F32, name="c_" + which)
+            c_sin = keep.tile([P, SLOTS, DH], F32, name="c_sin_" + which)
+            ab_engine.tensor_tensor(out=a[:], in0=cos_sb[:], in1=over_slots(gain[:]), op=ALU.mult)
+            ab_engine.tensor_tensor(out=b[:], in0=sin_sb[:], in1=over_slots(gain_rot[:]), op=ALU.mult)
+            nc.gpsimd.tensor_tensor(out=c[:], in0=cos_sb[:], in1=over_slots(shift), op=ALU.mult)
+            nc.gpsimd.tensor_tensor(out=c_sin[:], in0=sin_sb[:], in1=over_slots(shift_rot[:]), op=ALU.mult)
+            nc.gpsimd.tensor_tensor(out=c[:], in0=c[:], in1=c_sin[:], op=ALU.add)
+            return a, b, c
+
+        q_tables = rope_tables(vectors[:, 0, :], vectors[:, 1, :], nc.vector, "q")
+        k_tables = rope_tables(vectors[:, 2, :], vectors[:, 3, :], nc.gpsimd, "k")
+
+        x_words = x_sb[:].bitcast(F32)
+        grouped = keep.tile([P, SLOTS, PASSES, P, PACK], BF16, align_bytes=64)
+        x_codes = keep.tile([P, SLOTS, PASSES * P], U32, align_bytes=64)
+        x_planes = keep.tile([P, SLOTS, PASSES * P], U8, align_bytes=64)
+
+        def quantise_x(r):
+            for j in range(r * ROUND_SLOTS, (r + 1) * ROUND_SLOTS):
+                turned = psum_x.tile([P, PASSES * 2, P], F32)
+                for g in range(PASSES):
+                    for u in range(2):
+                        nc.tensor.transpose(
+                            turned[:, 2 * g + u, :],
+                            x_words[:, j, (K_PASS // 2) * g + u : (K_PASS // 2) * (g + 1) : 2],
+                            identity[:],
+                        )
+                nc.scalar.copy(
+                    out=grouped[:, j].bitcast(F32),
+                    in_=turned[:].rearrange("p (g u) r -> p g r u", u=2),
+                )
+            slots = slice(r * ROUND_SLOTS, (r + 1) * ROUND_SLOTS)
+            nc.vector.quantize_mx(
+                out=x_codes[:, slots, :].rearrange("p j w -> p (j w)").bitcast(FP8X4),
+                scales=x_planes[:, slots, :].rearrange("p j w -> p (j w)"),
+                in_=grouped[:, slots].rearrange("p j g r t -> p (j g r t)"),
+            )
+
+        def project(col0, j):
+            acc = psum_acc.tile([P, N_TILE], F32)
+            for g in range(PASSES):
+                nc.tensor.matmul_mx(
+                    out=acc[:],
+                    lhsT=x_codes[:, j, g * P : (g + 1) * P].bitcast(FP8X4),
+                    lhsT_scale=x_planes[:, j, g * P : (g + 1) * P],
+                    rhs=w_words[:, g, col0 : col0 + N_TILE].bitcast(FP8X4),
+                    rhs_scale=w_planes[4 * g : P, col0 : col0 + N_TILE],
+                    start=(g == 0),
+                    stop=(g == PASSES - 1),
+                )
+            return acc
+
+        def by_head(bank):
+            return bank[:].rearrange("p (h d) -> p h d", d=DH)
+
+        def store(result, dst, head0, r):
+            view = dst.rearrange("b h (p j) d -> p (b h) j d", j=SLOTS)
+            nc.sync.dma_start(
+                out=view[:, head0 : head0 + TILE_HEADS, r * ROUND_SLOTS : (r + 1) * ROUND_SLOTS, :],
+                in_=result[:],
+            )
+
+        def rotate_round(col0, r, tables):
+            a, b, c = tables
+            banks = [project(col0, r * ROUND_SLOTS + s) for s in range(ROUND_SLOTS)]
+
+            squares = work.tile([P, ROUND_HEADS, DH], F32)
+            sums = stats.tile([P, ROUND_HEADS], F32)
+            for s in range(ROUND_SLOTS):
+                for h in range(TILE_HEADS):
+                    i = s * TILE_HEADS + h
+                    nc.scalar.activation(
+                        out=squares[:, i, :],
+                        in_=banks[s][:, h * DH : (h + 1) * DH],
+                        func=ACT.Square,
+                        accum_out=sums[:, i : i + 1],
+                    )
+            rms = stats.tile([P, ROUND_HEADS], F32)
+            nc.scalar.activation(out=rms[:], in_=sums[:], func=ACT.Sqrt, bias=eps[:, 0:1], scale=1.0 / DH)
+
+            straight = work.tile([P, ROUND_SLOTS, TILE_HEADS, DH], F32, bufs=4)
+            crossed = work.tile([P, ROUND_SLOTS, TILE_HEADS, DH], F32)
+            for s in range(ROUND_SLOTS):
+                j = r * ROUND_SLOTS + s
+                u = by_head(banks[s])
+                nc.vector.tensor_tensor(
+                    out=straight[:, s],
+                    in0=u,
+                    in1=a[:, j, :].unsqueeze(1).to_broadcast([P, TILE_HEADS, DH]),
+                    op=ALU.mult,
+                )
+                for half in range(2):
+                    here = slice(half * HALF, (half + 1) * HALF)
+                    there = slice((1 - half) * HALF, (2 - half) * HALF)
+                    nc.vector.tensor_tensor(
+                        out=crossed[:, s, :, here],
+                        in0=u[:, :, there],
+                        in1=b[:, j, here].unsqueeze(1).to_broadcast([P, TILE_HEADS, HALF]),
+                        op=ALU.mult,
+                    )
+            rstd = stats.tile([P, ROUND_HEADS], F32)
+            nc.vector.reciprocal(out=rstd[:], in_=rms[:])
+            nc.vector.tensor_tensor(out=straight[:], in0=straight[:], in1=crossed[:], op=ALU.add)
+            return straight, rstd, c
+
+        def finish_round(rotated_round, dst, head0, r):
+            straight, rstd, c = rotated_round
+            result = results.tile([P, TILE_HEADS, ROUND_SLOTS, DH], F32)
+            for s in range(ROUND_SLOTS):
+                for h in range(TILE_HEADS):
+                    i = s * TILE_HEADS + h
+                    nc.scalar.activation(
+                        out=result[:, h, s, :], in_=straight[:, s, h, :], func=ACT.Copy, scale=rstd[:, i : i + 1]
+                    )
+            slots = slice(r * ROUND_SLOTS, (r + 1) * ROUND_SLOTS)
+            nc.gpsimd.tensor_tensor(
+                out=result[:],
+                in0=result[:],
+                in1=c[:, slots, :].unsqueeze(1).to_broadcast([P, TILE_HEADS, ROUND_SLOTS, DH]),
+                op=ALU.add,
+            )
+            store(result, dst, head0, r)
+
+        def value_round(r):
+            result = results.tile([P, TILE_HEADS, ROUND_SLOTS, DH], F32)
+            for s in range(ROUND_SLOTS):
+                bank = project(V_COL0, r * ROUND_SLOTS + s)
+                nc.scalar.copy(out=result[:, :, s, :], in_=by_head(bank))
+            store(result, out_2, 0, r)
+
+        tiles = [(out_0, t * TILE_HEADS, t * N_TILE, q_tables) for t in range(Q_HEADS // TILE_HEADS)]
+        tiles.append((out_1, 0, K_COL0, k_tables))
+        waiting = None
+        for t, (dst, head0, col0, tables) in enumerate(tiles):
+            for r in range(ROUNDS):
+                if t == 0:
+                    quantise_x(r)
+                rotated_round = rotate_round(col0, r, tables)
+                if waiting is not None:
+                    finish_round(*waiting)
+                waiting = (rotated_round, dst, head0, r)
+            if t < ROUNDS:
+                value_round(t)
+        finish_round(*waiting)

@@ -28,7 +28,7 @@ SLOTS = S // P
 N_TILE = 512
 TILE_HEADS = N_TILE // DH
 ROUND_SLOTS = 2
-ROUNDS = SLOTS // ROUND_SLOTS
+GROUPS = SLOTS // ROUND_SLOTS
 ROUND_HEADS = ROUND_SLOTS * TILE_HEADS
 
 Q_COLS = Q_HEADS * DH
@@ -63,8 +63,8 @@ def tile_groupqueryattention_pa_kernel(
         keep = ctx.enter_context(tc.tile_pool(name="keep", bufs=1))
         stats = ctx.enter_context(tc.tile_pool(name="stats", bufs=6))
         work = ctx.enter_context(tc.tile_pool(name="work", bufs=3))
-        results = ctx.enter_context(tc.tile_pool(name="results", bufs=6))
-        psum_x = ctx.enter_context(tc.psum_pool(name="psum_x", bufs=2))
+        results = ctx.enter_context(tc.tile_pool(name="results", bufs=4))
+        psum_c = ctx.enter_context(tc.psum_pool(name="psum_c", bufs=2))
         psum_acc = ctx.enter_context(tc.psum_pool(name="psum_acc", bufs=6))
 
         w_planes = keep.tile([P, N_ALL], U8, align_bytes=64)
@@ -73,6 +73,8 @@ def tile_groupqueryattention_pa_kernel(
         nc.vector.memset(eps[:], EPS)
         identity = keep.tile([P, P], F32)
         masks.make_identity(nc, identity[:])
+        identity_bf = keep.tile([P, P], BF16)
+        masks.make_identity(nc, identity_bf[:])
 
         vectors = keep.tile([P, 4, DH], BF16)
         for i, vector in enumerate((q_scale, q_shift, k_scale, k_shift)):
@@ -100,51 +102,22 @@ def tile_groupqueryattention_pa_kernel(
                     in_=scales[:, 4 * quadrant : 4 * quadrant + 4, :].bitcast(I32),
                 )
 
-        def load_words(words, col0, first, width):
-            for g in range(PASSES):
-                nc.sync.dma_start(
-                    out=w_words[:, g, col0 + first : col0 + first + width].bitcast(I32),
-                    in_=words[g].rearrange("p n t -> p (n t)")[:, PACK * first : PACK * (first + width)].bitcast(I32),
-                )
+        def load_words(words, col0, first):
+            nc.sync.dma_start(
+                out=w_words[:, :, col0 + first : col0 + first + N_TILE].bitcast(I32),
+                in_=words.rearrange("g p n t -> p g (n t)")[:, :, PACK * first : PACK * (first + N_TILE)].bitcast(I32),
+            )
 
         load_x(0)
         load_scales(wq_scales, 0)
-        load_words(wq_words, 0, 0, N_TILE)
-        for r in range(1, ROUNDS):
+        for t in range(Q_COLS // N_TILE):
+            load_words(wq_words, 0, t * N_TILE)
+        load_scales(wk_scales, K_COL0)
+        load_words(wk_words, K_COL0, 0)
+        for r in range(1, GROUPS):
             load_x(r)
         load_scales(wv_scales, V_COL0)
-        load_words(wv_words, V_COL0, 0, N_TILE)
-        load_words(wq_words, 0, N_TILE, Q_COLS - N_TILE)
-        load_scales(wk_scales, K_COL0)
-        load_words(wk_words, K_COL0, 0, N_TILE)
-
-        def rotated(vector, name):
-            rot = keep.tile([P, DH], F32, name=name)
-            nc.vector.tensor_scalar_mul(out=rot[:, 0:HALF], in0=vector[:, HALF:DH], scalar1=-1.0)
-            nc.vector.tensor_copy(out=rot[:, HALF:DH], in_=vector[:, 0:HALF])
-            return rot
-
-        def over_slots(vector):
-            return vector.unsqueeze(1).to_broadcast([P, SLOTS, DH])
-
-        def rope_tables(scale, shift, ab_engine, which):
-            gain = keep.tile([P, DH], F32, name="gain_" + which)
-            nc.vector.tensor_scalar_add(out=gain[:], in0=scale, scalar1=1.0)
-            gain_rot = rotated(gain[:], "gain_rot_" + which)
-            shift_rot = rotated(shift, "shift_rot_" + which)
-            a = keep.tile([P, SLOTS, DH], F32, name="a_" + which)
-            b = keep.tile([P, SLOTS, DH], F32, name="b_" + which)
-            c = keep.tile([P, SLOTS, DH], F32, name="c_" + which)
-            c_sin = keep.tile([P, SLOTS, DH], F32, name="c_sin_" + which)
-            ab_engine.tensor_tensor(out=a[:], in0=cos_sb[:], in1=over_slots(gain[:]), op=ALU.mult)
-            ab_engine.tensor_tensor(out=b[:], in0=sin_sb[:], in1=over_slots(gain_rot[:]), op=ALU.mult)
-            nc.gpsimd.tensor_tensor(out=c[:], in0=cos_sb[:], in1=over_slots(shift), op=ALU.mult)
-            nc.gpsimd.tensor_tensor(out=c_sin[:], in0=sin_sb[:], in1=over_slots(shift_rot[:]), op=ALU.mult)
-            nc.gpsimd.tensor_tensor(out=c[:], in0=c[:], in1=c_sin[:], op=ALU.add)
-            return a, b, c
-
-        q_tables = rope_tables(vectors[:, 0, :], vectors[:, 1, :], nc.vector, "q")
-        k_tables = rope_tables(vectors[:, 2, :], vectors[:, 3, :], nc.gpsimd, "k")
+        load_words(wv_words, V_COL0, 0)
 
         x_words = x_sb[:].bitcast(F32)
         grouped = keep.tile([P, SLOTS, PASSES, P, PACK], BF16, align_bytes=64)
@@ -153,7 +126,7 @@ def tile_groupqueryattention_pa_kernel(
 
         def quantise_x(r):
             for j in range(r * ROUND_SLOTS, (r + 1) * ROUND_SLOTS):
-                turned = psum_x.tile([P, PASSES * 2, P], F32)
+                turned = psum_acc.tile([P, PASSES * 2, P], F32, tag="acc")
                 for g in range(PASSES):
                     for u in range(2):
                         nc.tensor.transpose(
@@ -172,8 +145,63 @@ def tile_groupqueryattention_pa_kernel(
                 in_=grouped[:, slots].rearrange("p j g r t -> p (j g r t)"),
             )
 
+        diag_shift = keep.tile([P, 2 * DH], BF16)
+        diag_shift_rot = keep.tile([P, 2 * DH], BF16)
+
+        def rope_factors(scale, shift, which, table_engine):
+            name = ("q", "k")[which]
+            gain = keep.tile([P, DH], F32, name="gain_" + name)
+            nc.vector.tensor_scalar_add(out=gain[:], in0=scale, scalar1=1.0)
+            gain_signed = keep.tile([P, DH], F32, name="gain_signed_" + name)
+            nc.vector.tensor_copy(out=gain_signed[:, 0:HALF], in_=gain[:, 0:HALF])
+            nc.vector.tensor_scalar_mul(out=gain_signed[:, HALF:DH], in0=gain[:, HALF:DH], scalar1=-1.0)
+            shift_rot = keep.tile([P, DH], BF16, name="shift_rot_" + name)
+            nc.vector.tensor_scalar_mul(out=shift_rot[:, 0:HALF], in0=shift[:, HALF:DH], scalar1=-1.0)
+            nc.vector.tensor_copy(out=shift_rot[:, HALF:DH], in_=shift[:, 0:HALF])
+            columns = slice(which * DH, (which + 1) * DH)
+            nc.vector.tensor_tensor(out=diag_shift[:, columns], in0=identity_bf[:], in1=shift, op=ALU.mult)
+            nc.vector.tensor_tensor(out=diag_shift_rot[:, columns], in0=identity_bf[:], in1=shift_rot[:], op=ALU.mult)
+
+            ab = keep.tile([P, SLOTS, 2, DH], F32, name="ab_" + name)
+            table_engine.tensor_tensor(
+                out=ab[:, :, 0, :], in0=cos_sb[:], in1=gain[:].unsqueeze(1).to_broadcast([P, SLOTS, DH]), op=ALU.mult
+            )
+            for half in range(2):
+                here = slice(half * HALF, (half + 1) * HALF)
+                there = slice((1 - half) * HALF, (2 - half) * HALF)
+                table_engine.tensor_tensor(
+                    out=ab[:, :, 1, here],
+                    in0=sin_sb[:, :, there],
+                    in1=gain_signed[:, here].unsqueeze(1).to_broadcast([P, SLOTS, HALF]),
+                    op=ALU.mult,
+                )
+            return ab
+
+        def turned_table(table, name):
+            bank = psum_acc.tile([P, SLOTS, P], BF16, tag="acc")
+            for j in range(SLOTS):
+                nc.tensor.transpose(bank[:, j, :], table[:, j, :], identity_bf[:])
+            turned = keep.tile([P, SLOTS, P], BF16, name=name)
+            nc.scalar.copy(out=turned[:], in_=bank[:])
+            return turned
+
+        ab_q = rope_factors(vectors[:, 0, :], vectors[:, 1, :], 0, nc.vector)
+        quantise_x(0)
+        ab_k = rope_factors(vectors[:, 2, :], vectors[:, 3, :], 1, nc.gpsimd)
+        cos_t = turned_table(cos_sb, "cos_t")
+        sin_t = turned_table(sin_sb, "sin_t")
+
+        def shift_bank(r):
+            bank = psum_c.tile([P, ROUND_SLOTS, 2, DH], F32, tag="c")
+            for s in range(ROUND_SLOTS):
+                j = r * ROUND_SLOTS + s
+                both = bank[:, s].rearrange("p w d -> p (w d)")
+                nc.tensor.matmul(out=both, lhsT=cos_t[:, j, :], rhs=diag_shift[:], start=True, stop=False)
+                nc.tensor.matmul(out=both, lhsT=sin_t[:, j, :], rhs=diag_shift_rot[:], start=False, stop=True)
+            return bank
+
         def project(col0, j):
-            acc = psum_acc.tile([P, N_TILE], F32)
+            acc = psum_acc.tile([P, N_TILE], F32, tag="acc")
             for g in range(PASSES):
                 nc.tensor.matmul_mx(
                     out=acc[:],
@@ -196,11 +224,10 @@ def tile_groupqueryattention_pa_kernel(
                 in_=result[:],
             )
 
-        def rotate_round(col0, r, tables):
-            a, b, c = tables
+        def multiply_round(col0, r, ab):
             banks = [project(col0, r * ROUND_SLOTS + s) for s in range(ROUND_SLOTS)]
 
-            squares = work.tile([P, ROUND_HEADS, DH], F32)
+            squares = work.tile([P, ROUND_HEADS, DH], F32, bufs=2)
             sums = stats.tile([P, ROUND_HEADS], F32)
             for s in range(ROUND_SLOTS):
                 for h in range(TILE_HEADS):
@@ -214,45 +241,41 @@ def tile_groupqueryattention_pa_kernel(
             rms = stats.tile([P, ROUND_HEADS], F32)
             nc.scalar.activation(out=rms[:], in_=sums[:], func=ACT.Sqrt, bias=eps[:, 0:1], scale=1.0 / DH)
 
-            straight = work.tile([P, ROUND_SLOTS, TILE_HEADS, DH], F32, bufs=4)
-            crossed = work.tile([P, ROUND_SLOTS, TILE_HEADS, DH], F32)
+            products = work.tile([P, ROUND_SLOTS, 2, TILE_HEADS, DH], F32)
             for s in range(ROUND_SLOTS):
                 j = r * ROUND_SLOTS + s
-                u = by_head(banks[s])
                 nc.vector.tensor_tensor(
-                    out=straight[:, s],
-                    in0=u,
-                    in1=a[:, j, :].unsqueeze(1).to_broadcast([P, TILE_HEADS, DH]),
+                    out=products[:, s],
+                    in0=by_head(banks[s]).unsqueeze(1).to_broadcast([P, 2, TILE_HEADS, DH]),
+                    in1=ab[:, j].unsqueeze(2).to_broadcast([P, 2, TILE_HEADS, DH]),
                     op=ALU.mult,
                 )
-                for half in range(2):
-                    here = slice(half * HALF, (half + 1) * HALF)
-                    there = slice((1 - half) * HALF, (2 - half) * HALF)
-                    nc.vector.tensor_tensor(
-                        out=crossed[:, s, :, here],
-                        in0=u[:, :, there],
-                        in1=b[:, j, here].unsqueeze(1).to_broadcast([P, TILE_HEADS, HALF]),
-                        op=ALU.mult,
-                    )
             rstd = stats.tile([P, ROUND_HEADS], F32)
             nc.vector.reciprocal(out=rstd[:], in_=rms[:])
-            nc.vector.tensor_tensor(out=straight[:], in0=straight[:], in1=crossed[:], op=ALU.add)
-            return straight, rstd, c
+            return products, rstd
 
-        def finish_round(rotated_round, dst, head0, r):
-            straight, rstd, c = rotated_round
+        def add_round(products):
+            total = work.tile([P, ROUND_SLOTS, TILE_HEADS, DH], F32)
+            for half in range(2):
+                here = slice(half * HALF, (half + 1) * HALF)
+                there = slice((1 - half) * HALF, (2 - half) * HALF)
+                nc.gpsimd.tensor_tensor(
+                    out=total[:, :, :, here], in0=products[:, :, 0, :, here], in1=products[:, :, 1, :, there], op=ALU.add
+                )
+            return total
+
+        def finish_round(total, rstd, c_bank, which, dst, head0, r):
             result = results.tile([P, TILE_HEADS, ROUND_SLOTS, DH], F32)
             for s in range(ROUND_SLOTS):
                 for h in range(TILE_HEADS):
                     i = s * TILE_HEADS + h
                     nc.scalar.activation(
-                        out=result[:, h, s, :], in_=straight[:, s, h, :], func=ACT.Copy, scale=rstd[:, i : i + 1]
+                        out=result[:, h, s, :], in_=total[:, s, h, :], func=ACT.Copy, scale=rstd[:, i : i + 1]
                     )
-            slots = slice(r * ROUND_SLOTS, (r + 1) * ROUND_SLOTS)
-            nc.gpsimd.tensor_tensor(
+            nc.vector.tensor_tensor(
                 out=result[:],
                 in0=result[:],
-                in1=c[:, slots, :].unsqueeze(1).to_broadcast([P, TILE_HEADS, ROUND_SLOTS, DH]),
+                in1=c_bank[:, :, which, :].unsqueeze(1).to_broadcast([P, TILE_HEADS, ROUND_SLOTS, DH]),
                 op=ALU.add,
             )
             store(result, dst, head0, r)
@@ -264,17 +287,28 @@ def tile_groupqueryattention_pa_kernel(
                 nc.scalar.copy(out=result[:, :, s, :], in_=by_head(bank))
             store(result, out_2, 0, r)
 
-        tiles = [(out_0, t * TILE_HEADS, t * N_TILE, q_tables) for t in range(Q_HEADS // TILE_HEADS)]
-        tiles.append((out_1, 0, K_COL0, k_tables))
-        waiting = None
-        for t, (dst, head0, col0, tables) in enumerate(tiles):
-            for r in range(ROUNDS):
-                if t == 0:
-                    quantise_x(r)
-                rotated_round = rotate_round(col0, r, tables)
-                if waiting is not None:
-                    finish_round(*waiting)
-                waiting = (rotated_round, dst, head0, r)
-            if t < ROUNDS:
-                value_round(t)
-        finish_round(*waiting)
+        tiles = [(out_0, t * TILE_HEADS, t * N_TILE, ab_q, 0) for t in range(Q_HEADS // TILE_HEADS)]
+        tiles.append((out_1, 0, K_COL0, ab_k, 1))
+        PREPARE_AT = 3
+
+        jobs = [(r, t) for r in range(GROUPS) for t in range(len(tiles))]
+        c_banks = [shift_bank(0)]
+        multiplied = []
+        added = []
+        for m in range(len(jobs) + 2):
+            if m < len(jobs):
+                r, t = jobs[m]
+                multiplied.append(multiply_round(tiles[t][2], r, tiles[t][3]))
+                if t == PREPARE_AT and r + 1 < GROUPS:
+                    quantise_x(r + 1)
+                    c_banks.append(shift_bank(r + 1))
+            if 1 <= m <= len(jobs):
+                added.append(add_round(multiplied[m - 1][0]))
+            if m >= 2:
+                r, t = jobs[m - 2]
+                dst, head0, col0, ab, which = tiles[t]
+                finish_round(added[m - 2], multiplied[m - 2][1], c_banks[r], which, dst, head0, r)
+            if m == len(jobs):
+                for r in range(GROUPS - 1):
+                    value_round(r)
+        value_round(GROUPS - 1)

@@ -114,10 +114,10 @@ def tile_groupqueryattention_pa_kernel(
             load_words(wq_words, 0, t * N_TILE)
         load_scales(wk_scales, K_COL0)
         load_words(wk_words, K_COL0, 0)
-        for r in range(1, GROUPS):
-            load_x(r)
         load_scales(wv_scales, V_COL0)
         load_words(wv_words, V_COL0, 0)
+        for r in range(1, GROUPS):
+            load_x(r)
 
         x_words = x_sb[:].bitcast(F32)
         grouped = keep.tile([P, SLOTS, PASSES, P, PACK], BF16, align_bytes=64)
@@ -269,15 +269,14 @@ def tile_groupqueryattention_pa_kernel(
             for s in range(ROUND_SLOTS):
                 for h in range(TILE_HEADS):
                     i = s * TILE_HEADS + h
-                    nc.scalar.activation(
-                        out=result[:, h, s, :], in_=total[:, s, h, :], func=ACT.Copy, scale=rstd[:, i : i + 1]
+                    nc.vector.scalar_tensor_tensor(
+                        out=result[:, h, s, :],
+                        in0=total[:, s, h, :],
+                        scalar=rstd[:, i : i + 1],
+                        in1=c_bank[:, s, which, :],
+                        op0=ALU.mult,
+                        op1=ALU.add,
                     )
-            nc.vector.tensor_tensor(
-                out=result[:],
-                in0=result[:],
-                in1=c_bank[:, :, which, :].unsqueeze(1).to_broadcast([P, TILE_HEADS, ROUND_SLOTS, DH]),
-                op=ALU.add,
-            )
             store(result, dst, head0, r)
 
         def value_round(r):
@@ -302,13 +301,11 @@ def tile_groupqueryattention_pa_kernel(
                 if t == PREPARE_AT and r + 1 < GROUPS:
                     quantise_x(r + 1)
                     c_banks.append(shift_bank(r + 1))
+                if t == len(tiles) - 1:
+                    value_round(r)
             if 1 <= m <= len(jobs):
                 added.append(add_round(multiplied[m - 1][0]))
             if m >= 2:
                 r, t = jobs[m - 2]
                 dst, head0, col0, ab, which = tiles[t]
                 finish_round(added[m - 2], multiplied[m - 2][1], c_banks[r], which, dst, head0, r)
-            if m == len(jobs):
-                for r in range(GROUPS - 1):
-                    value_round(r)
-        value_round(GROUPS - 1)

@@ -30,6 +30,7 @@ TILE_HEADS = N_TILE // DH
 ROUND_SLOTS = 2
 GROUPS = SLOTS // ROUND_SLOTS
 ROUND_HEADS = ROUND_SLOTS * TILE_HEADS
+VECTOR_HEADS = 3
 
 Q_COLS = Q_HEADS * DH
 K_COL0 = Q_COLS
@@ -84,7 +85,7 @@ def tile_groupqueryattention_pa_kernel(
         nc.scalar.dma_start(out=cos_sb[:], in_=cos_thetas.rearrange("(p j) d -> p j d", j=SLOTS))
         nc.scalar.dma_start(out=sin_sb[:], in_=sin_thetas.rearrange("(p j) d -> p j d", j=SLOTS))
         table_warm = keep.tile([P, 1], F32)
-        nc.scalar.activation(out=table_warm[:], in_=eps[:], func=ACT.Sqrt)
+        nc.scalar.activation(out=table_warm[:], in_=eps[:], func=ACT.Abs_reciprocal_sqrt)
 
         x_sb = keep.tile([P, SLOTS, D], BF16)
         x_rows = x.flatten_outer_dims().rearrange("(p j) k -> p j k", j=SLOTS)
@@ -148,28 +149,28 @@ def tile_groupqueryattention_pa_kernel(
         diag_shift = keep.tile([P, 2 * DH], BF16)
         diag_shift_rot = keep.tile([P, 2 * DH], BF16)
 
-        def rope_factors(scale, shift, which, table_engine):
+        def rope_factors(scale, shift, which, engine):
             name = ("q", "k")[which]
             gain = keep.tile([P, DH], F32, name="gain_" + name)
-            nc.vector.tensor_scalar_add(out=gain[:], in0=scale, scalar1=1.0)
+            engine.tensor_scalar_add(out=gain[:], in0=scale, scalar1=1.0)
             gain_signed = keep.tile([P, DH], F32, name="gain_signed_" + name)
-            nc.vector.tensor_copy(out=gain_signed[:, 0:HALF], in_=gain[:, 0:HALF])
-            nc.vector.tensor_scalar_mul(out=gain_signed[:, HALF:DH], in0=gain[:, HALF:DH], scalar1=-1.0)
+            engine.tensor_copy(out=gain_signed[:, 0:HALF], in_=gain[:, 0:HALF])
+            engine.tensor_scalar_mul(out=gain_signed[:, HALF:DH], in0=gain[:, HALF:DH], scalar1=-1.0)
             shift_rot = keep.tile([P, DH], BF16, name="shift_rot_" + name)
-            nc.vector.tensor_scalar_mul(out=shift_rot[:, 0:HALF], in0=shift[:, HALF:DH], scalar1=-1.0)
-            nc.vector.tensor_copy(out=shift_rot[:, HALF:DH], in_=shift[:, 0:HALF])
+            engine.tensor_scalar_mul(out=shift_rot[:, 0:HALF], in0=shift[:, HALF:DH], scalar1=-1.0)
+            engine.tensor_copy(out=shift_rot[:, HALF:DH], in_=shift[:, 0:HALF])
             columns = slice(which * DH, (which + 1) * DH)
-            nc.vector.tensor_tensor(out=diag_shift[:, columns], in0=identity_bf[:], in1=shift, op=ALU.mult)
-            nc.vector.tensor_tensor(out=diag_shift_rot[:, columns], in0=identity_bf[:], in1=shift_rot[:], op=ALU.mult)
+            engine.tensor_tensor(out=diag_shift[:, columns], in0=identity_bf[:], in1=shift, op=ALU.mult)
+            engine.tensor_tensor(out=diag_shift_rot[:, columns], in0=identity_bf[:], in1=shift_rot[:], op=ALU.mult)
 
             ab = keep.tile([P, SLOTS, 2, DH], F32, name="ab_" + name)
-            table_engine.tensor_tensor(
+            engine.tensor_tensor(
                 out=ab[:, :, 0, :], in0=cos_sb[:], in1=gain[:].unsqueeze(1).to_broadcast([P, SLOTS, DH]), op=ALU.mult
             )
             for half in range(2):
                 here = slice(half * HALF, (half + 1) * HALF)
                 there = slice((1 - half) * HALF, (2 - half) * HALF)
-                table_engine.tensor_tensor(
+                engine.tensor_tensor(
                     out=ab[:, :, 1, here],
                     in0=sin_sb[:, :, there],
                     in1=gain_signed[:, here].unsqueeze(1).to_broadcast([P, SLOTS, HALF]),
@@ -198,7 +199,9 @@ def tile_groupqueryattention_pa_kernel(
                 both = bank[:, s].rearrange("p w d -> p (w d)")
                 nc.tensor.matmul(out=both, lhsT=cos_t[:, j, :], rhs=diag_shift[:], start=True, stop=False)
                 nc.tensor.matmul(out=both, lhsT=sin_t[:, j, :], rhs=diag_shift_rot[:], start=False, stop=True)
-            return bank
+            c_copy = work.tile([P, ROUND_SLOTS, 2, DH], F32, bufs=2)
+            nc.scalar.copy(out=c_copy[:], in_=bank[:])
+            return bank, c_copy
 
         def project(col0, j):
             acc = psum_acc.tile([P, N_TILE], F32, tag="acc")
@@ -238,8 +241,10 @@ def tile_groupqueryattention_pa_kernel(
                         func=ACT.Square,
                         accum_out=sums[:, i : i + 1],
                     )
-            rms = stats.tile([P, ROUND_HEADS], F32)
-            nc.scalar.activation(out=rms[:], in_=sums[:], func=ACT.Sqrt, bias=eps[:, 0:1], scale=1.0 / DH)
+            rstd = stats.tile([P, ROUND_HEADS], F32)
+            nc.scalar.activation(
+                out=rstd[:], in_=sums[:], func=ACT.Abs_reciprocal_sqrt, bias=eps[:, 0:1], scale=1.0 / DH
+            )
 
             products = work.tile([P, ROUND_SLOTS, 2, TILE_HEADS, DH], F32)
             for s in range(ROUND_SLOTS):
@@ -250,8 +255,6 @@ def tile_groupqueryattention_pa_kernel(
                     in1=ab[:, j].unsqueeze(2).to_broadcast([P, 2, TILE_HEADS, DH]),
                     op=ALU.mult,
                 )
-            rstd = stats.tile([P, ROUND_HEADS], F32)
-            nc.vector.reciprocal(out=rstd[:], in_=rms[:])
             return products, rstd
 
         def add_round(products):
@@ -264,19 +267,32 @@ def tile_groupqueryattention_pa_kernel(
                 )
             return total
 
-        def finish_round(total, rstd, c_bank, which, dst, head0, r):
+        def finish_round(total, rstd, c_pair, which, dst, head0, r):
+            c_bank, c_copy = c_pair
             result = results.tile([P, TILE_HEADS, ROUND_SLOTS, DH], F32)
             for s in range(ROUND_SLOTS):
                 for h in range(TILE_HEADS):
                     i = s * TILE_HEADS + h
-                    nc.vector.scalar_tensor_tensor(
-                        out=result[:, h, s, :],
-                        in0=total[:, s, h, :],
-                        scalar=rstd[:, i : i + 1],
-                        in1=c_bank[:, s, which, :],
-                        op0=ALU.mult,
-                        op1=ALU.add,
-                    )
+                    if h < VECTOR_HEADS:
+                        nc.vector.scalar_tensor_tensor(
+                            out=result[:, h, s, :],
+                            in0=total[:, s, h, :],
+                            scalar=rstd[:, i : i + 1],
+                            in1=c_bank[:, s, which, :],
+                            op0=ALU.mult,
+                            op1=ALU.add,
+                        )
+                    else:
+                        nc.scalar.activation(
+                            out=result[:, h, s, :], in_=total[:, s, h, :], func=ACT.Copy, scale=rstd[:, i : i + 1]
+                        )
+            others = result[:, VECTOR_HEADS:TILE_HEADS]
+            nc.gpsimd.tensor_tensor(
+                out=others,
+                in0=others,
+                in1=c_copy[:, :, which, :].unsqueeze(1).to_broadcast([P, TILE_HEADS - VECTOR_HEADS, ROUND_SLOTS, DH]),
+                op=ALU.add,
+            )
             store(result, dst, head0, r)
 
         def value_round(r):

@@ -30,7 +30,7 @@ TILE_HEADS = N_TILE // DH
 ROUND_SLOTS = 2
 GROUPS = SLOTS // ROUND_SLOTS
 ROUND_HEADS = ROUND_SLOTS * TILE_HEADS
-VECTOR_HEADS = 3
+FUSED_HEADS = 2
 
 Q_COLS = Q_HEADS * DH
 K_COL0 = Q_COLS
@@ -149,28 +149,28 @@ def tile_groupqueryattention_pa_kernel(
         diag_shift = keep.tile([P, 2 * DH], BF16)
         diag_shift_rot = keep.tile([P, 2 * DH], BF16)
 
-        def rope_factors(scale, shift, which, engine):
+        def rope_factors(scale, shift, which, table_engine):
             name = ("q", "k")[which]
             gain = keep.tile([P, DH], F32, name="gain_" + name)
-            engine.tensor_scalar_add(out=gain[:], in0=scale, scalar1=1.0)
+            nc.vector.tensor_scalar_add(out=gain[:], in0=scale, scalar1=1.0)
             gain_signed = keep.tile([P, DH], F32, name="gain_signed_" + name)
-            engine.tensor_copy(out=gain_signed[:, 0:HALF], in_=gain[:, 0:HALF])
-            engine.tensor_scalar_mul(out=gain_signed[:, HALF:DH], in0=gain[:, HALF:DH], scalar1=-1.0)
+            nc.vector.tensor_copy(out=gain_signed[:, 0:HALF], in_=gain[:, 0:HALF])
+            nc.vector.tensor_scalar_mul(out=gain_signed[:, HALF:DH], in0=gain[:, HALF:DH], scalar1=-1.0)
             shift_rot = keep.tile([P, DH], BF16, name="shift_rot_" + name)
-            engine.tensor_scalar_mul(out=shift_rot[:, 0:HALF], in0=shift[:, HALF:DH], scalar1=-1.0)
-            engine.tensor_copy(out=shift_rot[:, HALF:DH], in_=shift[:, 0:HALF])
+            nc.vector.tensor_scalar_mul(out=shift_rot[:, 0:HALF], in0=shift[:, HALF:DH], scalar1=-1.0)
+            nc.vector.tensor_copy(out=shift_rot[:, HALF:DH], in_=shift[:, 0:HALF])
             columns = slice(which * DH, (which + 1) * DH)
-            engine.tensor_tensor(out=diag_shift[:, columns], in0=identity_bf[:], in1=shift, op=ALU.mult)
-            engine.tensor_tensor(out=diag_shift_rot[:, columns], in0=identity_bf[:], in1=shift_rot[:], op=ALU.mult)
+            nc.vector.tensor_tensor(out=diag_shift[:, columns], in0=identity_bf[:], in1=shift, op=ALU.mult)
+            nc.vector.tensor_tensor(out=diag_shift_rot[:, columns], in0=identity_bf[:], in1=shift_rot[:], op=ALU.mult)
 
             ab = keep.tile([P, SLOTS, 2, DH], F32, name="ab_" + name)
-            engine.tensor_tensor(
+            table_engine.tensor_tensor(
                 out=ab[:, :, 0, :], in0=cos_sb[:], in1=gain[:].unsqueeze(1).to_broadcast([P, SLOTS, DH]), op=ALU.mult
             )
             for half in range(2):
                 here = slice(half * HALF, (half + 1) * HALF)
                 there = slice((1 - half) * HALF, (2 - half) * HALF)
-                engine.tensor_tensor(
+                table_engine.tensor_tensor(
                     out=ab[:, :, 1, here],
                     in0=sin_sb[:, :, there],
                     in1=gain_signed[:, here].unsqueeze(1).to_broadcast([P, SLOTS, HALF]),
@@ -199,9 +199,7 @@ def tile_groupqueryattention_pa_kernel(
                 both = bank[:, s].rearrange("p w d -> p (w d)")
                 nc.tensor.matmul(out=both, lhsT=cos_t[:, j, :], rhs=diag_shift[:], start=True, stop=False)
                 nc.tensor.matmul(out=both, lhsT=sin_t[:, j, :], rhs=diag_shift_rot[:], start=False, stop=True)
-            c_copy = work.tile([P, ROUND_SLOTS, 2, DH], F32, bufs=2)
-            nc.scalar.copy(out=c_copy[:], in_=bank[:])
-            return bank, c_copy
+            return bank
 
         def project(col0, j):
             acc = psum_acc.tile([P, N_TILE], F32, tag="acc")
@@ -267,13 +265,12 @@ def tile_groupqueryattention_pa_kernel(
                 )
             return total
 
-        def finish_round(total, rstd, c_pair, which, dst, head0, r):
-            c_bank, c_copy = c_pair
+        def finish_round(total, rstd, c_bank, which, dst, head0, r):
             result = results.tile([P, TILE_HEADS, ROUND_SLOTS, DH], F32)
             for s in range(ROUND_SLOTS):
                 for h in range(TILE_HEADS):
                     i = s * TILE_HEADS + h
-                    if h < VECTOR_HEADS:
+                    if h < FUSED_HEADS:
                         nc.vector.scalar_tensor_tensor(
                             out=result[:, h, s, :],
                             in0=total[:, s, h, :],
@@ -286,11 +283,11 @@ def tile_groupqueryattention_pa_kernel(
                         nc.scalar.activation(
                             out=result[:, h, s, :], in_=total[:, s, h, :], func=ACT.Copy, scale=rstd[:, i : i + 1]
                         )
-            others = result[:, VECTOR_HEADS:TILE_HEADS]
-            nc.gpsimd.tensor_tensor(
-                out=others,
-                in0=others,
-                in1=c_copy[:, :, which, :].unsqueeze(1).to_broadcast([P, TILE_HEADS - VECTOR_HEADS, ROUND_SLOTS, DH]),
+            scaled = result[:, FUSED_HEADS:TILE_HEADS]
+            nc.vector.tensor_tensor(
+                out=scaled,
+                in0=scaled,
+                in1=c_bank[:, :, which, :].unsqueeze(1).to_broadcast([P, TILE_HEADS - FUSED_HEADS, ROUND_SLOTS, DH]),
                 op=ALU.add,
             )
             store(result, dst, head0, r)

@@ -244,11 +244,11 @@ def tile_groupqueryattention_pa_kernel(
                 out=rstd[:], in_=sums[:], func=ACT.Abs_reciprocal_sqrt, bias=eps[:, 0:1], scale=1.0 / DH
             )
 
-            products = work.tile([P, ROUND_SLOTS, 2, TILE_HEADS, DH], F32)
+            products = work.tile([P, 2, ROUND_SLOTS, TILE_HEADS, DH], F32)
             for s in range(ROUND_SLOTS):
                 j = r * ROUND_SLOTS + s
                 nc.vector.tensor_tensor(
-                    out=products[:, s],
+                    out=products[:, :, s],
                     in0=by_head(banks[s]).unsqueeze(1).to_broadcast([P, 2, TILE_HEADS, DH]),
                     in1=ab[:, j].unsqueeze(2).to_broadcast([P, 2, TILE_HEADS, DH]),
                     op=ALU.mult,
@@ -257,12 +257,12 @@ def tile_groupqueryattention_pa_kernel(
 
         def add_round(products):
             total = work.tile([P, ROUND_SLOTS, TILE_HEADS, DH], F32)
-            for half in range(2):
-                here = slice(half * HALF, (half + 1) * HALF)
-                there = slice((1 - half) * HALF, (2 - half) * HALF)
-                nc.gpsimd.tensor_tensor(
-                    out=total[:, :, :, here], in0=products[:, :, 0, :, here], in1=products[:, :, 1, :, there], op=ALU.add
-                )
+            nc.gpsimd.tensor_tensor(
+                out=total[:].rearrange("p s h (a i) -> p (s h) a i", a=2),
+                in0=products[:, 0].rearrange("p s h (a i) -> p (s h) a i", a=2),
+                in1=products[:, 1].rearrange("p s h (a i) -> p (s h) a i", a=2)[:, :, ::-1, :],
+                op=ALU.add,
+            )
             return total
 
         def finish_round(total, rstd, c_bank, which, dst, head0, r):

@@ -77,9 +77,14 @@ def tile_groupqueryattention_pa_kernel(
         identity_bf = keep.tile([P, P], BF16)
         masks.make_identity(nc, identity_bf[:])
 
-        vectors = keep.tile([P, 4, DH], BF16)
+        vector_rows = keep.tile([P, 4 * DH], BF16)
+        nc.gpsimd.memset(vector_rows[:], 0.0)
         for i, vector in enumerate((q_scale, q_shift, k_scale, k_shift)):
-            nc.scalar.dma_start(out=vectors[:, i, :], in_=vector.partition_broadcast(P))
+            nc.scalar.dma_start(
+                out=vector_rows[0:1, i * DH : (i + 1) * DH], in_=vector.rearrange("(o d) -> o d", o=1)
+            )
+        ones = keep.tile([P, P], BF16)
+        nc.gpsimd.memset(ones[:], 1.0)
         cos_sb = keep.tile([P, SLOTS, DH], BF16)
         sin_sb = keep.tile([P, SLOTS, DH], BF16)
         nc.scalar.dma_start(out=cos_sb[:], in_=cos_thetas.rearrange("(p j) d -> p j d", j=SLOTS))
@@ -111,11 +116,11 @@ def tile_groupqueryattention_pa_kernel(
 
         load_x(0)
         load_scales(wq_scales, 0)
+        load_scales(wk_scales, K_COL0)
+        load_scales(wv_scales, V_COL0)
         for t in range(Q_COLS // N_TILE):
             load_words(wq_words, 0, t * N_TILE)
-        load_scales(wk_scales, K_COL0)
         load_words(wk_words, K_COL0, 0)
-        load_scales(wv_scales, V_COL0)
         load_words(wv_words, V_COL0, 0)
         for r in range(1, GROUPS):
             load_x(r)
@@ -185,6 +190,11 @@ def tile_groupqueryattention_pa_kernel(
             turned = keep.tile([P, SLOTS, P], BF16, name=name)
             nc.scalar.copy(out=turned[:], in_=bank[:])
             return turned
+
+        spread = psum_acc.tile([P, 4 * DH], F32, tag="acc")
+        nc.tensor.matmul(out=spread[:], lhsT=ones[:], rhs=vector_rows[:], start=True, stop=True)
+        vectors = keep.tile([P, 4, DH], F32)
+        nc.vector.tensor_copy(out=vectors[:].rearrange("p i d -> p (i d)"), in_=spread[:])
 
         ab_q = rope_factors(vectors[:, 0, :], vectors[:, 1, :], 0, nc.vector)
         quantise_x(0)

@@ -68,8 +68,16 @@ def tile_groupqueryattention_pa_kernel(
         psum_c = ctx.enter_context(tc.psum_pool(name="psum_c", bufs=2))
         psum_acc = ctx.enter_context(tc.psum_pool(name="psum_acc", bufs=6))
 
+        vector_rows = keep.tile([P, 4 * DH], BF16)
+        nc.vector.memset(vector_rows[:], 0.0)
+        for i, vector in enumerate((q_scale, q_shift, k_scale, k_shift)):
+            nc.scalar.dma_start(
+                out=vector_rows[0:1, i * DH : (i + 1) * DH], in_=vector.rearrange("(o d) -> o d", o=1)
+            )
         w_planes = keep.tile([P, N_ALL], U8, align_bytes=64)
         nc.vector.memset(w_planes[:].bitcast(I32), 0)
+        ones = keep.tile([P, P], BF16)
+        nc.vector.memset(ones[:], 1.0)
         eps = keep.tile([P, 1], F32)
         nc.vector.memset(eps[:], EPS)
         identity = keep.tile([P, P], F32)
@@ -77,14 +85,6 @@ def tile_groupqueryattention_pa_kernel(
         identity_bf = keep.tile([P, P], BF16)
         masks.make_identity(nc, identity_bf[:])
 
-        vector_rows = keep.tile([P, 4 * DH], BF16)
-        nc.gpsimd.memset(vector_rows[:], 0.0)
-        for i, vector in enumerate((q_scale, q_shift, k_scale, k_shift)):
-            nc.scalar.dma_start(
-                out=vector_rows[0:1, i * DH : (i + 1) * DH], in_=vector.rearrange("(o d) -> o d", o=1)
-            )
-        ones = keep.tile([P, P], BF16)
-        nc.gpsimd.memset(ones[:], 1.0)
         cos_sb = keep.tile([P, SLOTS, DH], BF16)
         sin_sb = keep.tile([P, SLOTS, DH], BF16)
         nc.scalar.dma_start(out=cos_sb[:], in_=cos_thetas.rearrange("(p j) d -> p j d", j=SLOTS))
@@ -193,8 +193,7 @@ def tile_groupqueryattention_pa_kernel(
 
         spread = psum_acc.tile([P, 4 * DH], F32, tag="acc")
         nc.tensor.matmul(out=spread[:], lhsT=ones[:], rhs=vector_rows[:], start=True, stop=True)
-        vectors = keep.tile([P, 4, DH], F32)
-        nc.vector.tensor_copy(out=vectors[:].rearrange("p i d -> p (i d)"), in_=spread[:])
+        vectors = spread[:].rearrange("p (i d) -> p i d", d=DH)
 
         ab_q = rope_factors(vectors[:, 0, :], vectors[:, 1, :], 0, nc.vector)
         quantise_x(0)

@@ -198,16 +198,15 @@ def tile_groupqueryattention_pa_kernel(
         ab_q = rope_factors(vectors[:, 0, :], vectors[:, 1, :], 0, nc.vector)
         quantise_x(0)
         ab_k = rope_factors(vectors[:, 2, :], vectors[:, 3, :], 1, nc.gpsimd)
-        cos_t = turned_table(cos_sb, "cos_t")
-        sin_t = turned_table(sin_sb, "sin_t")
+        turned_tables = []
 
         def shift_bank(r):
             bank = psum_c.tile([P, ROUND_SLOTS, 2, DH], F32, tag="c")
             for s in range(ROUND_SLOTS):
                 j = r * ROUND_SLOTS + s
                 both = bank[:, s].rearrange("p w d -> p (w d)")
-                nc.tensor.matmul(out=both, lhsT=cos_t[:, j, :], rhs=diag_shift[:], start=True, stop=False)
-                nc.tensor.matmul(out=both, lhsT=sin_t[:, j, :], rhs=diag_shift_rot[:], start=False, stop=True)
+                nc.tensor.matmul(out=both, lhsT=turned_tables[0][:, j, :], rhs=diag_shift[:], start=True, stop=False)
+                nc.tensor.matmul(out=both, lhsT=turned_tables[1][:, j, :], rhs=diag_shift_rot[:], start=False, stop=True)
             return bank
 
         def project(col0, j):
@@ -313,13 +312,18 @@ def tile_groupqueryattention_pa_kernel(
         PREPARE_AT = 3
 
         jobs = [(r, t) for r in range(GROUPS) for t in range(len(tiles))]
-        c_banks = [shift_bank(0)]
+        c_banks = []
         multiplied = []
         added = []
         for m in range(len(jobs) + 2):
             if m < len(jobs):
                 r, t = jobs[m]
                 multiplied.append(multiply_round(tiles[t][2], r, tiles[t][3]))
+                if m == 1:
+                    turned_tables.append(turned_table(cos_sb, "cos_t"))
+                    turned_tables.append(turned_table(sin_sb, "sin_t"))
+                if m == 2:
+                    c_banks.append(shift_bank(0))
                 if t == PREPARE_AT and r + 1 < GROUPS:
                     quantise_x(r + 1)
                     c_banks.append(shift_bank(r + 1))

@@ -31,6 +31,7 @@ ROUND_SLOTS = 2
 GROUPS = SLOTS // ROUND_SLOTS
 ROUND_HEADS = ROUND_SLOTS * TILE_HEADS
 FUSED_HEADS = 2
+WARM_UP = 8
 
 Q_COLS = Q_HEADS * DH
 K_COL0 = Q_COLS
@@ -78,6 +79,8 @@ def tile_groupqueryattention_pa_kernel(
         nc.vector.memset(w_planes[:].bitcast(I32), 0)
         ones = keep.tile([P, P], BF16)
         nc.vector.memset(ones[:], 1.0)
+        zeros = keep.tile([P, 4 * DH], BF16)
+        nc.vector.memset(zeros[:], 0.0)
         eps = keep.tile([P, 1], F32)
         nc.vector.memset(eps[:], EPS)
         identity = keep.tile([P, P], F32)
@@ -192,7 +195,9 @@ def tile_groupqueryattention_pa_kernel(
             return turned
 
         spread = psum_acc.tile([P, 4 * DH], F32, tag="acc")
-        nc.tensor.matmul(out=spread[:], lhsT=ones[:], rhs=vector_rows[:], start=True, stop=True)
+        for i in range(WARM_UP):
+            nc.tensor.matmul(out=spread[:], lhsT=ones[:], rhs=zeros[:], start=(i == 0), stop=False)
+        nc.tensor.matmul(out=spread[:], lhsT=ones[:], rhs=vector_rows[:], start=False, stop=True)
         vectors = spread[:].rearrange("p (i d) -> p i d", d=DH)
 
         ab_q = rope_factors(vectors[:, 0, :], vectors[:, 1, :], 0, nc.vector)

@@ -30,7 +30,9 @@ TILE_HEADS = N_TILE // DH
 ROUND_SLOTS = 2
 GROUPS = SLOTS // ROUND_SLOTS
 ROUND_HEADS = ROUND_SLOTS * TILE_HEADS
-FUSED_HEADS = 2
+TURNED = (1, 4)
+HALVES = 2
+HALF_PAIRS = ROUND_HEADS // HALVES
 WARM_UP = 8
 
 Q_COLS = Q_HEADS * DH
@@ -63,11 +65,13 @@ def tile_groupqueryattention_pa_kernel(
     nc = tc.nc
     with ExitStack() as ctx:
         keep = ctx.enter_context(tc.tile_pool(name="keep", bufs=1))
-        stats = ctx.enter_context(tc.tile_pool(name="stats", bufs=6))
-        work = ctx.enter_context(tc.tile_pool(name="work", bufs=3))
-        results = ctx.enter_context(tc.tile_pool(name="results", bufs=4))
-        psum_c = ctx.enter_context(tc.psum_pool(name="psum_c", bufs=2))
-        psum_acc = ctx.enter_context(tc.psum_pool(name="psum_acc", bufs=6))
+        stats = ctx.enter_context(tc.tile_pool(name="stats", bufs=16))
+        work = ctx.enter_context(tc.tile_pool(name="work", bufs=4))
+        results = ctx.enter_context(tc.tile_pool(name="results", bufs=6))
+        psum_c = ctx.enter_context(tc.psum_pool(name="psum_c", bufs=1))
+        psum_acc = ctx.enter_context(tc.psum_pool(name="psum_acc", bufs=4))
+        psum_brief = ctx.enter_context(tc.psum_pool(name="psum_brief", bufs=2))
+        psum_sum = ctx.enter_context(tc.psum_pool(name="psum_sum", bufs=1))
 
         vector_rows = keep.tile([P, 4 * DH], BF16)
         nc.vector.memset(vector_rows[:], 0.0)
@@ -87,6 +91,11 @@ def tile_groupqueryattention_pa_kernel(
         masks.make_identity(nc, identity[:])
         identity_bf = keep.tile([P, P], BF16)
         masks.make_identity(nc, identity_bf[:])
+        exchange = keep.tile([P, P], F32)
+        nc.gpsimd.tensor_copy(
+            out=exchange[:].rearrange("p (a i) -> p a i", a=2),
+            in_=identity[:].rearrange("p (a i) -> p a i", a=2)[:, ::-1, :],
+        )
 
         cos_sb = keep.tile([P, SLOTS, DH], BF16)
         sin_sb = keep.tile([P, SLOTS, DH], BF16)
@@ -129,60 +138,52 @@ def tile_groupqueryattention_pa_kernel(
             load_x(r)
 
         x_words = x_sb[:].bitcast(F32)
-        grouped = keep.tile([P, SLOTS, PASSES, P, PACK], BF16, align_bytes=64)
-        x_codes = keep.tile([P, SLOTS, PASSES * P], U32, align_bytes=64)
-        x_planes = keep.tile([P, SLOTS, PASSES * P], U8, align_bytes=64)
+        grouped = keep.tile([P, GROUPS, PASSES, ROUND_SLOTS * P, PACK], BF16, align_bytes=64)
+        x_codes = keep.tile([P, GROUPS, PASSES, ROUND_SLOTS * P], U32, align_bytes=64)
+        x_planes = keep.tile([P, GROUPS, PASSES, ROUND_SLOTS * P], U8, align_bytes=64)
+
+        def turn_x(r, s):
+            turned = psum_brief.tile([P, PASSES * 2, P], F32, tag="brief")
+            for g in range(PASSES):
+                for u in range(2):
+                    nc.tensor.transpose(
+                        turned[:, 2 * g + u, :],
+                        x_words[:, r * ROUND_SLOTS + s, (K_PASS // 2) * g + u : (K_PASS // 2) * (g + 1) : 2],
+                        identity[:],
+                    )
+            nc.scalar.copy(
+                out=grouped[:, r, :, s * P : (s + 1) * P, :].bitcast(F32),
+                in_=turned[:].rearrange("p (g u) r -> p g r u", u=2),
+            )
 
         def quantise_x(r):
-            for j in range(r * ROUND_SLOTS, (r + 1) * ROUND_SLOTS):
-                turned = psum_acc.tile([P, PASSES * 2, P], F32, tag="acc")
-                for g in range(PASSES):
-                    for u in range(2):
-                        nc.tensor.transpose(
-                            turned[:, 2 * g + u, :],
-                            x_words[:, j, (K_PASS // 2) * g + u : (K_PASS // 2) * (g + 1) : 2],
-                            identity[:],
-                        )
-                nc.scalar.copy(
-                    out=grouped[:, j].bitcast(F32),
-                    in_=turned[:].rearrange("p (g u) r -> p g r u", u=2),
-                )
-            slots = slice(r * ROUND_SLOTS, (r + 1) * ROUND_SLOTS)
             nc.vector.quantize_mx(
-                out=x_codes[:, slots, :].rearrange("p j w -> p (j w)").bitcast(FP8X4),
-                scales=x_planes[:, slots, :].rearrange("p j w -> p (j w)"),
-                in_=grouped[:, slots].rearrange("p j g r t -> p (j g r t)"),
+                out=x_codes[:, r].rearrange("p g w -> p (g w)").bitcast(FP8X4),
+                scales=x_planes[:, r].rearrange("p g w -> p (g w)"),
+                in_=grouped[:, r].rearrange("p g w t -> p (g w t)"),
             )
 
-        diag_shift = keep.tile([P, 2 * DH], BF16)
-        diag_shift_rot = keep.tile([P, 2 * DH], BF16)
+        sin_x = keep.tile([P, SLOTS, DH], BF16)
+        nc.vector.tensor_copy(out=sin_x[:, :, 0:HALF], in_=sin_sb[:, :, HALF:DH])
+        nc.vector.tensor_scalar_mul(out=sin_x[:, :, HALF:DH], in0=sin_sb[:, :, 0:HALF], scalar1=-1.0)
 
-        def rope_factors(scale, shift, which, table_engine):
-            name = ("q", "k")[which]
-            gain = keep.tile([P, DH], F32, name="gain_" + name)
+        diag_shift = keep.tile([P, 2, DH], BF16)
+        diag_shift_x = keep.tile([P, 2, DH], BF16)
+
+        def shift_factors(shift, which):
+            nc.vector.tensor_tensor(out=diag_shift[:, which, :], in0=identity_bf[:], in1=shift, op=ALU.mult)
+            nc.vector.tensor_copy(
+                out=diag_shift_x[:, which, :].rearrange("p (a i) -> p a i", a=2),
+                in_=diag_shift[:, which, :].rearrange("p (a i) -> p a i", a=2)[:, ::-1, :],
+            )
+
+        def upright_tables(scale):
+            gain = keep.tile([P, DH], F32)
             nc.vector.tensor_scalar_add(out=gain[:], in0=scale, scalar1=1.0)
-            gain_signed = keep.tile([P, DH], F32, name="gain_signed_" + name)
-            nc.vector.tensor_copy(out=gain_signed[:, 0:HALF], in_=gain[:, 0:HALF])
-            nc.vector.tensor_scalar_mul(out=gain_signed[:, HALF:DH], in0=gain[:, HALF:DH], scalar1=-1.0)
-            shift_rot = keep.tile([P, DH], BF16, name="shift_rot_" + name)
-            nc.vector.tensor_scalar_mul(out=shift_rot[:, 0:HALF], in0=shift[:, HALF:DH], scalar1=-1.0)
-            nc.vector.tensor_copy(out=shift_rot[:, HALF:DH], in_=shift[:, 0:HALF])
-            columns = slice(which * DH, (which + 1) * DH)
-            nc.vector.tensor_tensor(out=diag_shift[:, columns], in0=identity_bf[:], in1=shift, op=ALU.mult)
-            nc.vector.tensor_tensor(out=diag_shift_rot[:, columns], in0=identity_bf[:], in1=shift_rot[:], op=ALU.mult)
-
-            ab = keep.tile([P, SLOTS, 2, DH], F32, name="ab_" + name)
-            table_engine.tensor_tensor(
-                out=ab[:, :, 0, :], in0=cos_sb[:], in1=gain[:].unsqueeze(1).to_broadcast([P, SLOTS, DH]), op=ALU.mult
-            )
-            for half in range(2):
-                here = slice(half * HALF, (half + 1) * HALF)
-                there = slice((1 - half) * HALF, (2 - half) * HALF)
-                table_engine.tensor_tensor(
-                    out=ab[:, :, 1, here],
-                    in0=sin_sb[:, :, there],
-                    in1=gain_signed[:, here].unsqueeze(1).to_broadcast([P, SLOTS, HALF]),
-                    op=ALU.mult,
+            ab = keep.tile([P, SLOTS, 2, DH], F32)
+            for i, table in enumerate((cos_sb, sin_x)):
+                nc.vector.tensor_tensor(
+                    out=ab[:, :, i, :], in0=table[:], in1=gain[:].unsqueeze(1).to_broadcast([P, SLOTS, DH]), op=ALU.mult
                 )
             return ab
 
@@ -199,37 +200,82 @@ def tile_groupqueryattention_pa_kernel(
             nc.tensor.matmul(out=spread[:], lhsT=ones[:], rhs=zeros[:], start=(i == 0), stop=False)
         nc.tensor.matmul(out=spread[:], lhsT=ones[:], rhs=vector_rows[:], start=False, stop=True)
         vectors = spread[:].rearrange("p (i d) -> p i d", d=DH)
+        columns_bank = psum_acc.tile([P, 2, P], BF16, tag="acc")
+        for which in range(2):
+            nc.tensor.transpose(columns_bank[:, which, :], vector_rows[:, 2 * which * DH : (2 * which + 1) * DH], identity_bf[:])
 
-        ab_q = rope_factors(vectors[:, 0, :], vectors[:, 1, :], 0, nc.vector)
+        ab_q = upright_tables(vectors[:, 0, :])
+        gain_cols = keep.tile([P, 2], F32)
+        nc.vector.tensor_scalar_add(out=gain_cols[:], in0=columns_bank[:, :, 0], scalar1=1.0)
+        for s in range(ROUND_SLOTS):
+            turn_x(0, s)
         quantise_x(0)
-        ab_k = rope_factors(vectors[:, 2, :], vectors[:, 3, :], 1, nc.gpsimd)
-        turned_tables = []
+        shift_factors(vectors[:, 1, :], 0)
+        shift_factors(vectors[:, 3, :], 1)
+        turned_tables = (turned_table(cos_sb, "cos_t"), turned_table(sin_x, "sin_x_t"))
+
+        ab_turned = []
+        for which in range(2):
+            ab = keep.tile([P, 2, S], F32, name="ab_turned_" + ("q", "k")[which])
+            for i in range(2):
+                nc.gpsimd.tensor_scalar(
+                    out=ab[:, i, :],
+                    in0=turned_tables[i][:].rearrange("p j q -> p (j q)"),
+                    scalar1=gain_cols[:, which : which + 1],
+                    scalar2=0.0,
+                    op0=ALU.mult,
+                    op1=ALU.add,
+                )
+            ab_turned.append(ab)
+
+        def shift_products(out, j, diag_columns):
+            for i, diag in enumerate((diag_shift, diag_shift_x)):
+                nc.tensor.matmul(
+                    out=out,
+                    lhsT=turned_tables[i][:, j, :],
+                    rhs=diag[:, diag_columns, :].rearrange("p w d -> p (w d)"),
+                    start=(i == 0),
+                    stop=(i == 1),
+                )
+
+        shifts = keep.tile([P, GROUPS, ROUND_SLOTS, 2, DH], F32)
+
+        def shift_copy(r):
+            bank = psum_brief.tile([P, ROUND_SLOTS, 2 * DH], F32, tag="brief", name="shift_bank")
+            for s in range(ROUND_SLOTS):
+                shift_products(bank[:, s], r * ROUND_SLOTS + s, slice(0, 2))
+            nc.scalar.copy(out=shifts[:, r].rearrange("p s w d -> p s (w d)"), in_=bank[:])
 
         def shift_bank(r):
-            bank = psum_c.tile([P, ROUND_SLOTS, 2, DH], F32, tag="c")
-            for s in range(ROUND_SLOTS):
-                j = r * ROUND_SLOTS + s
-                both = bank[:, s].rearrange("p w d -> p (w d)")
-                nc.tensor.matmul(out=both, lhsT=turned_tables[0][:, j, :], rhs=diag_shift[:], start=True, stop=False)
-                nc.tensor.matmul(out=both, lhsT=turned_tables[1][:, j, :], rhs=diag_shift_rot[:], start=False, stop=True)
+            bank = psum_c.tile([P, 2 * ROUND_SLOTS, DH], F32, tag="c")
+            for s in range(2 * ROUND_SLOTS):
+                shift_products(bank[:, s], r * ROUND_SLOTS + s, slice(0, 1))
             return bank
 
-        def project(col0, j):
-            acc = psum_acc.tile([P, N_TILE], F32, tag="acc")
+        def product(out, r, s, columns):
+            here = slice(s * P, (s + 1) * P)
             for g in range(PASSES):
                 nc.tensor.matmul_mx(
-                    out=acc[:],
-                    lhsT=x_codes[:, j, g * P : (g + 1) * P].bitcast(FP8X4),
-                    lhsT_scale=x_planes[:, j, g * P : (g + 1) * P],
-                    rhs=w_words[:, g, col0 : col0 + N_TILE].bitcast(FP8X4),
-                    rhs_scale=w_planes[4 * g : P, col0 : col0 + N_TILE],
+                    out=out,
+                    lhsT=x_codes[:, r, g, here].bitcast(FP8X4),
+                    lhsT_scale=x_planes[:, r, g, here],
+                    rhs=w_words[:, g, columns].bitcast(FP8X4),
+                    rhs_scale=w_planes[4 * g : P, columns],
                     start=(g == 0),
                     stop=(g == PASSES - 1),
                 )
-            return acc
 
-        def by_head(bank):
-            return bank[:].rearrange("p (h d) -> p h d", d=DH)
+        def product_turned(out, r, columns):
+            for g in range(PASSES):
+                nc.tensor.matmul_mx(
+                    out=out,
+                    lhsT=w_words[:, g, columns].bitcast(FP8X4),
+                    lhsT_scale=w_planes[4 * g : P, columns],
+                    rhs=x_codes[:, r, g, :].bitcast(FP8X4),
+                    rhs_scale=x_planes[:, r, g, :],
+                    start=(g == 0),
+                    stop=(g == PASSES - 1),
+                )
 
         def store(result, dst, head0, r):
             view = dst.rearrange("b h (p j) d -> p (b h) j d", j=SLOTS)
@@ -238,105 +284,181 @@ def tile_groupqueryattention_pa_kernel(
                 in_=result[:],
             )
 
-        def multiply_round(col0, r, ab):
-            banks = [project(col0, r * ROUND_SLOTS + s) for s in range(ROUND_SLOTS)]
+        def value_half(r, s, result):
+            bank = psum_brief.tile([P, TILE_HEADS, DH], F32, tag="brief", name="value_bank")
+            product(bank[:].rearrange("p h d -> p (h d)"), r, s, slice(V_COL0, V_COL0 + N_TILE))
+            nc.scalar.copy(out=result[:, :, s, :], in_=bank[:])
+            if s == ROUND_SLOTS - 1:
+                store(result, out_2, 0, r)
 
-            squares = work.tile([P, ROUND_HEADS, DH], F32, bufs=2)
-            sums = stats.tile([P, ROUND_HEADS], F32)
-            for s in range(ROUND_SLOTS):
-                for h in range(TILE_HEADS):
-                    i = s * TILE_HEADS + h
-                    nc.scalar.activation(
-                        out=squares[:, i, :],
-                        in_=banks[s][:, h * DH : (h + 1) * DH],
-                        func=ACT.Square,
-                        accum_out=sums[:, i : i + 1],
-                    )
-            rstd = stats.tile([P, ROUND_HEADS], F32)
+        tiles = [(out_0, t * TILE_HEADS, t * N_TILE, 0) for t in range(Q_HEADS // TILE_HEADS)]
+        tiles.append((out_1, 0, K_COL0, 1))
+        c_banks = {}
+        rounds = {}
+
+        def step_matmul(r, t, h):
+            state = rounds.setdefault((r, t), {"rstd": {}})
+            col0 = tiles[t][2]
+            acc = psum_acc.tile([P, N_TILE], F32, tag="acc")
+            if t in TURNED:
+                pair0 = col0 + h * 2 * DH
+                brief = psum_brief.tile([P, ROUND_SLOTS, 2, DH], F32, tag="brief", name="square_bank")
+                for s in range(ROUND_SLOTS):
+                    product(brief[:, s].rearrange("p h d -> p (h d)"), r, s, slice(pair0, pair0 + 2 * DH))
+                state["squared", h] = brief[:].rearrange("p s h d -> p (s h) d")
+                for i in range(2):
+                    product_turned(acc[:, i * 2 * P : (i + 1) * 2 * P], r, slice(pair0 + i * DH, pair0 + (i + 1) * DH))
+            else:
+                product(acc[:], r, h, slice(col0, col0 + N_TILE))
+                state["squared", h] = acc[:].rearrange("p (h d) -> p h d", d=DH)
+            state["acc", h] = acc
+
+        def step_squares(r, t, h):
+            state = rounds[r, t]
+            squares = work.tile([P, HALF_PAIRS, DH], F32, bufs=2)
+            sums = stats.tile([P, HALF_PAIRS], F32)
+            for i in range(HALF_PAIRS):
+                nc.scalar.activation(
+                    out=squares[:, i, :], in_=state["squared", h][:, i, :], func=ACT.Square, accum_out=sums[:, i : i + 1]
+                )
+            rstd = stats.tile([P, HALF_PAIRS], F32)
             nc.scalar.activation(
                 out=rstd[:], in_=sums[:], func=ACT.Abs_reciprocal_sqrt, bias=eps[:, 0:1], scale=1.0 / DH
             )
+            state["rstd"][h] = rstd
 
-            products = work.tile([P, 2, ROUND_SLOTS, TILE_HEADS, DH], F32)
-            for s in range(ROUND_SLOTS):
-                j = r * ROUND_SLOTS + s
+        def step_multiply(r, t, h):
+            state = rounds[r, t]
+            acc = state["acc", h]
+            if t in TURNED:
+                pair = acc[:].rearrange("p (h q) -> p h q", h=2)
+                products = work.tile([P, 2, 2, ROUND_SLOTS * P], F32, name="products_turned")
+                table = ab_turned[tiles[t][3]][:, :, r * ROUND_SLOTS * P : (r + 1) * ROUND_SLOTS * P]
                 nc.vector.tensor_tensor(
-                    out=products[:, :, s],
-                    in0=by_head(banks[s]).unsqueeze(1).to_broadcast([P, 2, TILE_HEADS, DH]),
-                    in1=ab[:, j].unsqueeze(2).to_broadcast([P, 2, TILE_HEADS, DH]),
+                    out=products[:],
+                    in0=pair.unsqueeze(1).to_broadcast([P, 2, 2, ROUND_SLOTS * P]),
+                    in1=table.unsqueeze(2).to_broadcast([P, 2, 2, ROUND_SLOTS * P]),
                     op=ALU.mult,
                 )
-            return products, rstd
+                state["products", h] = products
+            else:
+                if h == 0:
+                    products = work.tile([P, 2, ROUND_SLOTS, TILE_HEADS, DH], F32)
+                    state["products"] = products
+                nc.vector.tensor_tensor(
+                    out=state["products"][:, :, h],
+                    in0=acc[:].rearrange("p (h d) -> p h d", d=DH).unsqueeze(1).to_broadcast([P, 2, TILE_HEADS, DH]),
+                    in1=ab_q[:, r * ROUND_SLOTS + h].unsqueeze(2).to_broadcast([P, 2, TILE_HEADS, DH]),
+                    op=ALU.mult,
+                )
 
-        def add_round(products):
-            total = work.tile([P, ROUND_SLOTS, TILE_HEADS, DH], F32)
-            nc.gpsimd.tensor_tensor(
-                out=total[:].rearrange("p s h (a i) -> p (s h) a i", a=2),
-                in0=products[:, 0].rearrange("p s h (a i) -> p (s h) a i", a=2),
-                in1=products[:, 1].rearrange("p s h (a i) -> p (s h) a i", a=2)[:, :, ::-1, :],
-                op=ALU.add,
-            )
-            return total
+        def step_add(r, t, h):
+            state = rounds[r, t]
+            if t in TURNED:
+                bank = psum_sum.tile([P, 2, ROUND_SLOTS, DH], F32, tag="sum")
+                products = state["products", h]
+                for i in range(2):
+                    for s in range(ROUND_SLOTS):
+                        for which, order in enumerate((identity, exchange)):
+                            nc.tensor.matmul(
+                                out=bank[:, i, s, :],
+                                lhsT=products[:, which, i, s * P : (s + 1) * P],
+                                rhs=order[:],
+                                is_transpose=True,
+                                start=(which == 0),
+                                stop=(which == 1),
+                            )
+                state["sum", h] = bank
+            elif h == HALVES - 1:
+                products = state["products"]
+                total = work.tile([P, ROUND_SLOTS, TILE_HEADS, DH], F32)
+                nc.gpsimd.tensor_tensor(
+                    out=total[:].rearrange("p s h (a i) -> p (s h) a i", a=2),
+                    in0=products[:, 0].rearrange("p s h (a i) -> p (s h) a i", a=2),
+                    in1=products[:, 1].rearrange("p s h (a i) -> p (s h) a i", a=2)[:, :, ::-1, :],
+                    op=ALU.add,
+                )
+                state["total"] = total
 
-        def finish_round(total, rstd, c_bank, which, dst, head0, r):
-            result = results.tile([P, TILE_HEADS, ROUND_SLOTS, DH], F32)
-            for s in range(ROUND_SLOTS):
-                for h in range(TILE_HEADS):
-                    i = s * TILE_HEADS + h
-                    if h < FUSED_HEADS:
+        def step_finish(r, t, h):
+            state = rounds[r, t]
+            dst, head0, col0, which = tiles[t]
+            if t in TURNED:
+                if h == 0:
+                    result = results.tile([P, TILE_HEADS, ROUND_SLOTS, DH], F32)
+                    state["result"] = result
+                result = state["result"]
+                for i in range(2):
+                    for s in range(ROUND_SLOTS):
+                        j = s * 2 + i
+                        nc.scalar.activation(
+                            out=result[:, 2 * h + i, s, :],
+                            in_=state["sum", h][:, i, s, :],
+                            func=ACT.Copy,
+                            scale=state["rstd"][h][:, j : j + 1],
+                        )
+                if h == HALVES - 1:
+                    nc.gpsimd.tensor_tensor(
+                        out=result[:],
+                        in0=result[:],
+                        in1=shifts[:, r, :, which, :].unsqueeze(1).to_broadcast([P, TILE_HEADS, ROUND_SLOTS, DH]),
+                        op=ALU.add,
+                    )
+                    store(result, dst, head0, r)
+            elif h == HALVES - 1:
+                result = results.tile([P, TILE_HEADS, ROUND_SLOTS, DH], F32)
+                for s in range(ROUND_SLOTS):
+                    for i in range(TILE_HEADS):
                         nc.vector.scalar_tensor_tensor(
-                            out=result[:, h, s, :],
-                            in0=total[:, s, h, :],
-                            scalar=rstd[:, i : i + 1],
-                            in1=c_bank[:, s, which, :],
+                            out=result[:, i, s, :],
+                            in0=state["total"][:, s, i, :],
+                            scalar=state["rstd"][s][:, i : i + 1],
+                            in1=c_banks[r // 2][:, (r % 2) * ROUND_SLOTS + s, :],
                             op0=ALU.mult,
                             op1=ALU.add,
                         )
-                    else:
-                        nc.scalar.activation(
-                            out=result[:, h, s, :], in_=total[:, s, h, :], func=ACT.Copy, scale=rstd[:, i : i + 1]
-                        )
-            scaled = result[:, FUSED_HEADS:TILE_HEADS]
-            nc.vector.tensor_tensor(
-                out=scaled,
-                in0=scaled,
-                in1=c_bank[:, :, which, :].unsqueeze(1).to_broadcast([P, TILE_HEADS - FUSED_HEADS, ROUND_SLOTS, DH]),
-                op=ALU.add,
-            )
-            store(result, dst, head0, r)
+                store(result, dst, head0, r)
 
-        def value_round(r):
-            result = results.tile([P, TILE_HEADS, ROUND_SLOTS, DH], F32)
-            for s in range(ROUND_SLOTS):
-                bank = project(V_COL0, r * ROUND_SLOTS + s)
-                nc.scalar.copy(out=result[:, :, s, :], in_=by_head(bank))
-            store(result, out_2, 0, r)
-
-        tiles = [(out_0, t * TILE_HEADS, t * N_TILE, ab_q, 0) for t in range(Q_HEADS // TILE_HEADS)]
-        tiles.append((out_1, 0, K_COL0, ab_k, 1))
-        PREPARE_AT = 3
-
-        jobs = [(r, t) for r in range(GROUPS) for t in range(len(tiles))]
-        c_banks = []
-        multiplied = []
-        added = []
-        for m in range(len(jobs) + 2):
-            if m < len(jobs):
-                r, t = jobs[m]
-                multiplied.append(multiply_round(tiles[t][2], r, tiles[t][3]))
-                if m == 1:
-                    turned_tables.append(turned_table(cos_sb, "cos_t"))
-                    turned_tables.append(turned_table(sin_sb, "sin_t"))
-                if m == 2:
-                    c_banks.append(shift_bank(0))
-                if t == PREPARE_AT and r + 1 < GROUPS:
-                    quantise_x(r + 1)
-                    c_banks.append(shift_bank(r + 1))
-                if t == len(tiles) - 1:
-                    value_round(r)
-            if 1 <= m <= len(jobs):
-                added.append(add_round(multiplied[m - 1][0]))
-            if m >= 2:
-                r, t = jobs[m - 2]
-                dst, head0, col0, ab, which = tiles[t]
-                finish_round(added[m - 2], multiplied[m - 2][1], c_banks[r], which, dst, head0, r)
+        order = [(r, t, h) for r in range(GROUPS) for t in range(len(tiles)) for h in range(HALVES)]
+        per_group = len(tiles) * HALVES
+        AHEAD = 2
+        ADD_LAG = 2
+        FINISH_LAG = 5
+        TURN_X_AT = 5
+        VALUES_AT = (4, 8)
+        values = {}
+        for m in range(-AHEAD, len(order) + FINISH_LAG):
+            if m - ADD_LAG in range(len(order)):
+                step_add(*order[m - ADD_LAG])
+            if m + AHEAD in range(len(order)):
+                step_matmul(*order[m + AHEAD])
+            if m + 1 in range(len(order)):
+                step_squares(*order[m + 1])
+            if m in range(len(order)):
+                step_multiply(*order[m])
+            if m - ADD_LAG in range(len(order)) and order[m - ADD_LAG][1] in TURNED:
+                step_finish(*order[m - ADD_LAG])
+            if m - FINISH_LAG in range(len(order)) and order[m - FINISH_LAG][1] not in TURNED:
+                step_finish(*order[m - FINISH_LAG])
+            if m in range(len(order)):
+                r = m // per_group
+                if m == 0:
+                    shift_copy(0)
+                    c_banks[0] = shift_bank(0)
+                if m % per_group in VALUES_AT:
+                    s = VALUES_AT.index(m % per_group)
+                    if s == 0:
+                        result = results.tile([P, TILE_HEADS, ROUND_SLOTS, DH], F32)
+                        values[r] = result
+                    value_half(r, s, values[r])
+            ahead = m + AHEAD
+            if ahead in range(len(order)) and ahead // per_group + 1 < GROUPS:
+                r = ahead // per_group + 1
+                s = ahead % per_group - TURN_X_AT
+                if s in range(ROUND_SLOTS):
+                    turn_x(r, s)
+                if s == ROUND_SLOTS - 1:
+                    quantise_x(r)
+                    shift_copy(r)
+            if m == 2 * per_group + 3:
+                c_banks[1] = shift_bank(2)

@@ -30,7 +30,8 @@ TILE_HEADS = N_TILE // DH
 ROUND_SLOTS = 2
 GROUPS = SLOTS // ROUND_SLOTS
 ROUND_HEADS = ROUND_SLOTS * TILE_HEADS
-TURNED = (1, 4)
+TURNED = (2, 4)
+LAST_UPRIGHT = 3
 HALVES = 2
 HALF_PAIRS = ROUND_HEADS // HALVES
 WARM_UP = 8
@@ -277,11 +278,13 @@ def tile_groupqueryattention_pa_kernel(
                     stop=(g == PASSES - 1),
                 )
 
-        def store(result, dst, head0, r):
+        def store(result, dst, head0, r, heads=slice(0, TILE_HEADS), slots=slice(0, ROUND_SLOTS)):
             view = dst.rearrange("b h (p j) d -> p (b h) j d", j=SLOTS)
             nc.sync.dma_start(
-                out=view[:, head0 : head0 + TILE_HEADS, r * ROUND_SLOTS : (r + 1) * ROUND_SLOTS, :],
-                in_=result[:],
+                out=view[
+                    :, head0 + heads.start : head0 + heads.stop, r * ROUND_SLOTS + slots.start : r * ROUND_SLOTS + slots.stop, :
+                ],
+                in_=result[:, heads, slots, :],
             )
 
         def value_half(r, s, result):
@@ -293,6 +296,7 @@ def tile_groupqueryattention_pa_kernel(
 
         tiles = [(out_0, t * TILE_HEADS, t * N_TILE, 0) for t in range(Q_HEADS // TILE_HEADS)]
         tiles.append((out_1, 0, K_COL0, 1))
+        order = [(r, t, h) for r in range(GROUPS) for t in range(len(tiles)) for h in range(HALVES)]
         c_banks = {}
         rounds = {}
 
@@ -352,33 +356,46 @@ def tile_groupqueryattention_pa_kernel(
                     op=ALU.mult,
                 )
 
+        def finished_slots(r, t, h):
+            if (r, t) == (GROUPS - 1, LAST_UPRIGHT):
+                return slice(h, h + 1)
+            return slice(0, ROUND_SLOTS) if h == HALVES - 1 else None
+
         def step_add(r, t, h):
             state = rounds[r, t]
             if t in TURNED:
-                bank = psum_sum.tile([P, 2, ROUND_SLOTS, DH], F32, tag="sum")
+                if (r, t, h) == order[-1]:
+                    bank = psum_acc.tile([P, 2, ROUND_SLOTS, DH], F32, tag="acc", name="last_sum")
+                else:
+                    bank = psum_sum.tile([P, 2, ROUND_SLOTS, DH], F32, tag="sum")
                 products = state["products", h]
                 for i in range(2):
                     for s in range(ROUND_SLOTS):
-                        for which, order in enumerate((identity, exchange)):
+                        for which, permutation in enumerate((identity, exchange)):
                             nc.tensor.matmul(
                                 out=bank[:, i, s, :],
                                 lhsT=products[:, which, i, s * P : (s + 1) * P],
-                                rhs=order[:],
+                                rhs=permutation[:],
                                 is_transpose=True,
                                 start=(which == 0),
                                 stop=(which == 1),
                             )
                 state["sum", h] = bank
-            elif h == HALVES - 1:
+            else:
+                slots = finished_slots(r, t, h)
+                if slots is None:
+                    return
+                if "total" not in state:
+                    total = work.tile([P, ROUND_SLOTS, TILE_HEADS, DH], F32)
+                    state["total"] = total
+                total = state["total"]
                 products = state["products"]
-                total = work.tile([P, ROUND_SLOTS, TILE_HEADS, DH], F32)
                 nc.gpsimd.tensor_tensor(
-                    out=total[:].rearrange("p s h (a i) -> p (s h) a i", a=2),
-                    in0=products[:, 0].rearrange("p s h (a i) -> p (s h) a i", a=2),
-                    in1=products[:, 1].rearrange("p s h (a i) -> p (s h) a i", a=2)[:, :, ::-1, :],
+                    out=total[:, slots].rearrange("p s h (a i) -> p (s h) a i", a=2),
+                    in0=products[:, 0, slots].rearrange("p s h (a i) -> p (s h) a i", a=2),
+                    in1=products[:, 1, slots].rearrange("p s h (a i) -> p (s h) a i", a=2)[:, :, ::-1, :],
                     op=ALU.add,
                 )
-                state["total"] = total
 
         def step_finish(r, t, h):
             state = rounds[r, t]
@@ -388,6 +405,21 @@ def tile_groupqueryattention_pa_kernel(
                     result = results.tile([P, TILE_HEADS, ROUND_SLOTS, DH], F32)
                     state["result"] = result
                 result = state["result"]
+                heads = slice(2 * h, 2 * h + 2)
+                if (r, t, h) == order[-1]:
+                    for i in range(2):
+                        for s in range(ROUND_SLOTS):
+                            j = s * 2 + i
+                            nc.vector.scalar_tensor_tensor(
+                                out=result[:, 2 * h + i, s, :],
+                                in0=state["sum", h][:, i, s, :],
+                                scalar=state["rstd"][h][:, j : j + 1],
+                                in1=shifts[:, r, s, which, :],
+                                op0=ALU.mult,
+                                op1=ALU.add,
+                            )
+                    store(result, dst, head0, r, heads=heads)
+                    return
                 for i in range(2):
                     for s in range(ROUND_SLOTS):
                         j = s * 2 + i
@@ -397,17 +429,27 @@ def tile_groupqueryattention_pa_kernel(
                             func=ACT.Copy,
                             scale=state["rstd"][h][:, j : j + 1],
                         )
-                if h == HALVES - 1:
+                very_last = (r, t) == order[-1][:2]
+                if very_last or h == HALVES - 1:
+                    done = heads if very_last else slice(0, TILE_HEADS)
                     nc.gpsimd.tensor_tensor(
-                        out=result[:],
-                        in0=result[:],
-                        in1=shifts[:, r, :, which, :].unsqueeze(1).to_broadcast([P, TILE_HEADS, ROUND_SLOTS, DH]),
+                        out=result[:, done],
+                        in0=result[:, done],
+                        in1=shifts[:, r, :, which, :]
+                        .unsqueeze(1)
+                        .to_broadcast([P, done.stop - done.start, ROUND_SLOTS, DH]),
                         op=ALU.add,
                     )
-                    store(result, dst, head0, r)
-            elif h == HALVES - 1:
-                result = results.tile([P, TILE_HEADS, ROUND_SLOTS, DH], F32)
-                for s in range(ROUND_SLOTS):
+                    store(result, dst, head0, r, heads=done)
+            else:
+                slots = finished_slots(r, t, h)
+                if slots is None:
+                    return
+                if "result" not in state:
+                    result = results.tile([P, TILE_HEADS, ROUND_SLOTS, DH], F32)
+                    state["result"] = result
+                result = state["result"]
+                for s in range(slots.start, slots.stop):
                     for i in range(TILE_HEADS):
                         nc.vector.scalar_tensor_tensor(
                             out=result[:, i, s, :],
@@ -417,40 +459,46 @@ def tile_groupqueryattention_pa_kernel(
                             op0=ALU.mult,
                             op1=ALU.add,
                         )
-                store(result, dst, head0, r)
+                store(result, dst, head0, r, slots=slots)
 
-        order = [(r, t, h) for r in range(GROUPS) for t in range(len(tiles)) for h in range(HALVES)]
         per_group = len(tiles) * HALVES
-        AHEAD = 2
-        ADD_LAG = 2
-        FINISH_LAG = 5
-        TURN_X_AT = 5
-        VALUES_AT = (4, 8)
+        AHEAD = 1
+        ADD_LAG = 3
+        FINISH_LAG = 7
+        LAST_FINISH_LAG = 4
+        SHIFT_AT = 2
+        TURN_X_AT = 6
+        VALUES_AT = (1, 7)
         values = {}
         for m in range(-AHEAD, len(order) + FINISH_LAG):
+            if m in range(len(order)):
+                step_multiply(*order[m])
             if m - ADD_LAG in range(len(order)):
                 step_add(*order[m - ADD_LAG])
             if m + AHEAD in range(len(order)):
                 step_matmul(*order[m + AHEAD])
-            if m + 1 in range(len(order)):
-                step_squares(*order[m + 1])
-            if m in range(len(order)):
-                step_multiply(*order[m])
             if m - ADD_LAG in range(len(order)) and order[m - ADD_LAG][1] in TURNED:
                 step_finish(*order[m - ADD_LAG])
-            if m - FINISH_LAG in range(len(order)) and order[m - FINISH_LAG][1] not in TURNED:
-                step_finish(*order[m - FINISH_LAG])
-            if m in range(len(order)):
+            for lag in (FINISH_LAG, LAST_FINISH_LAG):
+                if m - lag in range(len(order)):
+                    r, t, h = order[m - lag]
+                    very_last = (r, t) == (GROUPS - 1, LAST_UPRIGHT)
+                    if t not in TURNED and lag == (LAST_FINISH_LAG if very_last else FINISH_LAG):
+                        step_finish(r, t, h)
+                        if (r, t, h) == (1, LAST_UPRIGHT, HALVES - 1):
+                            c_banks[1] = shift_bank(2)
+            if m + AHEAD in range(len(order)):
+                step_squares(*order[m + AHEAD])
+            if m == SHIFT_AT:
+                shift_copy(0)
+                c_banks[0] = shift_bank(0)
+            if m in range(len(order)) and m % per_group in VALUES_AT:
                 r = m // per_group
-                if m == 0:
-                    shift_copy(0)
-                    c_banks[0] = shift_bank(0)
-                if m % per_group in VALUES_AT:
-                    s = VALUES_AT.index(m % per_group)
-                    if s == 0:
-                        result = results.tile([P, TILE_HEADS, ROUND_SLOTS, DH], F32)
-                        values[r] = result
-                    value_half(r, s, values[r])
+                s = VALUES_AT.index(m % per_group)
+                if s == 0:
+                    result = results.tile([P, TILE_HEADS, ROUND_SLOTS, DH], F32)
+                    values[r] = result
+                value_half(r, s, values[r])
             ahead = m + AHEAD
             if ahead in range(len(order)) and ahead // per_group + 1 < GROUPS:
                 r = ahead // per_group + 1
@@ -460,5 +508,3 @@ def tile_groupqueryattention_pa_kernel(
                 if s == ROUND_SLOTS - 1:
                     quantise_x(r)
                     shift_copy(r)
-            if m == 2 * per_group + 3:
-                c_banks[1] = shift_bank(2)

@@ -356,7 +356,7 @@ def tile_groupqueryattention_pa_kernel(
                     op=ALU.mult,
                 )
 
-        def finished_slots(r, t, h):
+        def joint_slots(r, t, h):
             if (r, t) == (GROUPS - 1, LAST_UPRIGHT):
                 return slice(h, h + 1)
             return slice(0, ROUND_SLOTS) if h == HALVES - 1 else None
@@ -382,7 +382,7 @@ def tile_groupqueryattention_pa_kernel(
                             )
                 state["sum", h] = bank
             else:
-                slots = finished_slots(r, t, h)
+                slots = joint_slots(r, t, h)
                 if slots is None:
                     return
                 if "total" not in state:
@@ -442,33 +442,32 @@ def tile_groupqueryattention_pa_kernel(
                     )
                     store(result, dst, head0, r, heads=done)
             else:
-                slots = finished_slots(r, t, h)
-                if slots is None:
-                    return
                 if "result" not in state:
                     result = results.tile([P, TILE_HEADS, ROUND_SLOTS, DH], F32)
                     state["result"] = result
                 result = state["result"]
-                for s in range(slots.start, slots.stop):
-                    for i in range(TILE_HEADS):
-                        nc.vector.scalar_tensor_tensor(
-                            out=result[:, i, s, :],
-                            in0=state["total"][:, s, i, :],
-                            scalar=state["rstd"][s][:, i : i + 1],
-                            in1=c_banks[r // 2][:, (r % 2) * ROUND_SLOTS + s, :],
-                            op0=ALU.mult,
-                            op1=ALU.add,
-                        )
-                store(result, dst, head0, r, slots=slots)
+                for i in range(TILE_HEADS):
+                    nc.vector.scalar_tensor_tensor(
+                        out=result[:, i, h, :],
+                        in0=state["total"][:, h, i, :],
+                        scalar=state["rstd"][h][:, i : i + 1],
+                        in1=c_banks[r // 2][:, (r % 2) * ROUND_SLOTS + h, :],
+                        op0=ALU.mult,
+                        op1=ALU.add,
+                    )
+                slots = joint_slots(r, t, h)
+                if slots is not None:
+                    store(result, dst, head0, r, slots=slots)
 
         per_group = len(tiles) * HALVES
         AHEAD = 1
         ADD_LAG = 3
-        FINISH_LAG = 7
+        FINISH_LAG = 8
         LAST_FINISH_LAG = 4
         SHIFT_AT = 2
-        TURN_X_AT = 6
-        VALUES_AT = (1, 7)
+        TURN_X_AT = 7
+        value_steps = {(r + 1) * per_group + s: (r, s) for r in range(GROUPS - 1) for s in range(ROUND_SLOTS)}
+        value_steps.update({(GROUPS - 1) * per_group + ROUND_SLOTS + s: (GROUPS - 1, s) for s in range(ROUND_SLOTS)})
         values = {}
         for m in range(-AHEAD, len(order) + FINISH_LAG):
             if m in range(len(order)):
@@ -492,9 +491,8 @@ def tile_groupqueryattention_pa_kernel(
             if m == SHIFT_AT:
                 shift_copy(0)
                 c_banks[0] = shift_bank(0)
-            if m in range(len(order)) and m % per_group in VALUES_AT:
-                r = m // per_group
-                s = VALUES_AT.index(m % per_group)
+            if m in value_steps:
+                r, s = value_steps[m]
                 if s == 0:
                     result = results.tile([P, TILE_HEADS, ROUND_SLOTS, DH], F32)
                     values[r] = result

from contextlib import ExitStack

import concourse.masks as masks
import concourse.mybir as mybir

F32 = mybir.dt.float32
BF16 = mybir.dt.bfloat16
U8 = mybir.dt.uint8
U32 = mybir.dt.uint32
I32 = mybir.dt.int32
FP8X4 = mybir.dt.float8_e4m3fn_x4
ACT = mybir.ActivationFunctionType
ALU = mybir.AluOpType

P = 128
S = 1024
D = 1024
DH = 128
HALF = DH // 2
Q_HEADS = 16
KV_HEADS = 4
EPS = 1e-6

PACK = 4
K_PASS = P * PACK
PASSES = D // K_PASS
SLOTS = S // P
N_TILE = 512
TILE_HEADS = N_TILE // DH
ROUND_SLOTS = 2
GROUPS = SLOTS // ROUND_SLOTS
ROUND_HEADS = ROUND_SLOTS * TILE_HEADS
TURNED = (2, 4)
LAST_UPRIGHT = 3
HALVES = 2
HALF_PAIRS = ROUND_HEADS // HALVES
WARM_UP = 8

Q_COLS = Q_HEADS * DH
K_COL0 = Q_COLS
V_COL0 = Q_COLS + KV_HEADS * DH
N_ALL = Q_COLS + 2 * KV_HEADS * DH

FLOPS = 2 * S * D * N_ALL


def tile_groupqueryattention_pa_kernel(
    tc,
    x,
    sin_thetas,
    cos_thetas,
    wq_words,
    wq_scales,
    wk_words,
    wk_scales,
    wv_words,
    wv_scales,
    q_scale,
    q_shift,
    k_scale,
    k_shift,
    out_0,
    out_1,
    out_2,
):
    nc = tc.nc
    with ExitStack() as ctx:
        keep = ctx.enter_context(tc.tile_pool(name="keep", bufs=1))
        stats = ctx.enter_context(tc.tile_pool(name="stats", bufs=16))
        work = ctx.enter_context(tc.tile_pool(name="work", bufs=4))
        results = ctx.enter_context(tc.tile_pool(name="results", bufs=6))
        psum_c = ctx.enter_context(tc.psum_pool(name="psum_c", bufs=1))
        psum_acc = ctx.enter_context(tc.psum_pool(name="psum_acc", bufs=4))
        psum_brief = ctx.enter_context(tc.psum_pool(name="psum_brief", bufs=2))
        psum_sum = ctx.enter_context(tc.psum_pool(name="psum_sum", bufs=1))

        vector_rows = keep.tile([P, 4 * DH], BF16)
        nc.vector.memset(vector_rows[:], 0.0)
        for i, vector in enumerate((q_scale, q_shift, k_scale, k_shift)):
            nc.scalar.dma_start(
                out=vector_rows[0:1, i * DH : (i + 1) * DH], in_=vector.rearrange("(o d) -> o d", o=1)
            )
        w_planes = keep.tile([P, N_ALL], U8, align_bytes=64)
        nc.vector.memset(w_planes[:].bitcast(I32), 0)
        ones = keep.tile([P, P], BF16)
        nc.vector.memset(ones[:], 1.0)
        zeros = keep.tile([P, 4 * DH], BF16)
        nc.vector.memset(zeros[:], 0.0)
        eps = keep.tile([P, 1], F32)
        nc.vector.memset(eps[:], EPS)
        identity = keep.tile([P, P], F32)
        masks.make_identity(nc, identity[:])
        identity_bf = keep.tile([P, P], BF16)
        masks.make_identity(nc, identity_bf[:])
        exchange = keep.tile([P, P], F32)
        nc.gpsimd.tensor_copy(
            out=exchange[:].rearrange("p (a i) -> p a i", a=2),
            in_=identity[:].rearrange("p (a i) -> p a i", a=2)[:, ::-1, :],
        )

        cos_sb = keep.tile([P, SLOTS, DH], BF16)
        sin_sb = keep.tile([P, SLOTS, DH], BF16)
        nc.scalar.dma_start(out=cos_sb[:], in_=cos_thetas.rearrange("(p j) d -> p j d", j=SLOTS))
        nc.scalar.dma_start(out=sin_sb[:], in_=sin_thetas.rearrange("(p j) d -> p j d", j=SLOTS))
        table_warm = keep.tile([P, 1], F32)
        nc.scalar.activation(out=table_warm[:], in_=eps[:], func=ACT.Abs_reciprocal_sqrt)

        x_sb = keep.tile([P, SLOTS, D], BF16)
        x_rows = x.flatten_outer_dims().rearrange("(p j) k -> p j k", j=SLOTS)
        w_words = keep.tile([P, PASSES, N_ALL], U32, align_bytes=64)

        def load_x(r):
            slots = slice(r * ROUND_SLOTS, (r + 1) * ROUND_SLOTS)
            nc.sync.dma_start(out=x_sb[:, slots, :], in_=x_rows[:, slots, :])

        def load_scales(scales, col0):
            width = scales.shape[2]
            for quadrant in range(4):
                nc.sync.dma_start(
                    out=w_planes[32 * quadrant : 32 * quadrant + 4 * PASSES, col0 : col0 + width].bitcast(I32),
                    in_=scales[:, 4 * quadrant : 4 * quadrant + 4, :].bitcast(I32),
                )

        def load_words(words, col0, first):
            nc.sync.dma_start(
                out=w_words[:, :, col0 + first : col0 + first + N_TILE].bitcast(I32),
                in_=words.rearrange("g p n t -> p g (n t)")[:, :, PACK * first : PACK * (first + N_TILE)].bitcast(I32),
            )

        load_x(0)
        load_scales(wq_scales, 0)
        load_scales(wk_scales, K_COL0)
        load_scales(wv_scales, V_COL0)
        for t in range(Q_COLS // N_TILE):
            load_words(wq_words, 0, t * N_TILE)
        load_words(wk_words, K_COL0, 0)
        load_words(wv_words, V_COL0, 0)
        for r in range(1, GROUPS):
            load_x(r)

        x_words = x_sb[:].bitcast(F32)
        grouped = keep.tile([P, GROUPS, PASSES, ROUND_SLOTS * P, PACK], BF16, align_bytes=64)
        x_codes = keep.tile([P, GROUPS, PASSES, ROUND_SLOTS * P], U32, align_bytes=64)
        x_planes = keep.tile([P, GROUPS, PASSES, ROUND_SLOTS * P], U8, align_bytes=64)

        def turn_x(r, s):
            turned = psum_brief.tile([P, PASSES * 2, P], F32, tag="brief")
            for g in range(PASSES):
                for u in range(2):
                    nc.tensor.transpose(
                        turned[:, 2 * g + u, :],
                        x_words[:, r * ROUND_SLOTS + s, (K_PASS // 2) * g + u : (K_PASS // 2) * (g + 1) : 2],
                        identity[:],
                    )
            nc.scalar.copy(
                out=grouped[:, r, :, s * P : (s + 1) * P, :].bitcast(F32),
                in_=turned[:].rearrange("p (g u) r -> p g r u", u=2),
            )

        def quantise_x(r):
            nc.vector.quantize_mx(
                out=x_codes[:, r].rearrange("p g w -> p (g w)").bitcast(FP8X4),
                scales=x_planes[:, r].rearrange("p g w -> p (g w)"),
                in_=grouped[:, r].rearrange("p g w t -> p (g w t)"),
            )

        sin_x = keep.tile([P, SLOTS, DH], BF16)
        nc.vector.tensor_copy(out=sin_x[:, :, 0:HALF], in_=sin_sb[:, :, HALF:DH])
        nc.vector.tensor_scalar_mul(out=sin_x[:, :, HALF:DH], in0=sin_sb[:, :, 0:HALF], scalar1=-1.0)

        diag_shift = keep.tile([P, 2, DH], BF16)
        diag_shift_x = keep.tile([P, 2, DH], BF16)

        def shift_factors(shift, which):
            nc.vector.tensor_tensor(out=diag_shift[:, which, :], in0=identity_bf[:], in1=shift, op=ALU.mult)
            nc.vector.tensor_copy(
                out=diag_shift_x[:, which, :].rearrange("p (a i) -> p a i", a=2),
                in_=diag_shift[:, which, :].rearrange("p (a i) -> p a i", a=2)[:, ::-1, :],
            )

        def upright_tables(scale):
            gain = keep.tile([P, DH], F32)
            nc.vector.tensor_scalar_add(out=gain[:], in0=scale, scalar1=1.0)
            ab = keep.tile([P, SLOTS, 2, DH], F32)
            for i, table in enumerate((cos_sb, sin_x)):
                nc.vector.tensor_tensor(
                    out=ab[:, :, i, :], in0=table[:], in1=gain[:].unsqueeze(1).to_broadcast([P, SLOTS, DH]), op=ALU.mult
                )
            return ab

        def turned_table(table, name):
            bank = psum_acc.tile([P, SLOTS, P], BF16, tag="acc")
            for j in range(SLOTS):
                nc.tensor.transpose(bank[:, j, :], table[:, j, :], identity_bf[:])
            turned = keep.tile([P, SLOTS, P], BF16, name=name)
            nc.scalar.copy(out=turned[:], in_=bank[:])
            return turned

        spread = psum_acc.tile([P, 4 * DH], F32, tag="acc")
        for i in range(WARM_UP):
            nc.tensor.matmul(out=spread[:], lhsT=ones[:], rhs=zeros[:], start=(i == 0), stop=False)
        nc.tensor.matmul(out=spread[:], lhsT=ones[:], rhs=vector_rows[:], start=False, stop=True)
        vectors = spread[:].rearrange("p (i d) -> p i d", d=DH)
        columns_bank = psum_acc.tile([P, 2, P], BF16, tag="acc")
        for which in range(2):
            nc.tensor.transpose(columns_bank[:, which, :], vector_rows[:, 2 * which * DH : (2 * which + 1) * DH], identity_bf[:])

        ab_q = upright_tables(vectors[:, 0, :])
        gain_cols = keep.tile([P, 2], F32)
        nc.vector.tensor_scalar_add(out=gain_cols[:], in0=columns_bank[:, :, 0], scalar1=1.0)
        for s in range(ROUND_SLOTS):
            turn_x(0, s)
        quantise_x(0)
        shift_factors(vectors[:, 1, :], 0)
        shift_factors(vectors[:, 3, :], 1)
        turned_tables = (turned_table(cos_sb, "cos_t"), turned_table(sin_x, "sin_x_t"))

        ab_turned = []
        for which in range(2):
            ab = keep.tile([P, 2, S], F32, name="ab_turned_" + ("q", "k")[which])
            for i in range(2):
                nc.gpsimd.tensor_scalar(
                    out=ab[:, i, :],
                    in0=turned_tables[i][:].rearrange("p j q -> p (j q)"),
                    scalar1=gain_cols[:, which : which + 1],
                    scalar2=0.0,
                    op0=ALU.mult,
                    op1=ALU.add,
                )
            ab_turned.append(ab)

        def shift_products(out, j, diag_columns):
            for i, diag in enumerate((diag_shift, diag_shift_x)):
                nc.tensor.matmul(
                    out=out,
                    lhsT=turned_tables[i][:, j, :],
                    rhs=diag[:, diag_columns, :].rearrange("p w d -> p (w d)"),
                    start=(i == 0),
                    stop=(i == 1),
                )

        shifts = keep.tile([P, GROUPS, ROUND_SLOTS, 2, DH], F32)

        def shift_copy(r):
            bank = psum_brief.tile([P, ROUND_SLOTS, 2 * DH], F32, tag="brief", name="shift_bank")
            for s in range(ROUND_SLOTS):
                shift_products(bank[:, s], r * ROUND_SLOTS + s, slice(0, 2))
            nc.scalar.copy(out=shifts[:, r].rearrange("p s w d -> p s (w d)"), in_=bank[:])

        def shift_bank(r):
            bank = psum_c.tile([P, 2 * ROUND_SLOTS, DH], F32, tag="c")
            for s in range(2 * ROUND_SLOTS):
                shift_products(bank[:, s], r * ROUND_SLOTS + s, slice(0, 1))
            return bank

        def product(out, r, s, columns):
            here = slice(s * P, (s + 1) * P)
            for g in range(PASSES):
                nc.tensor.matmul_mx(
                    out=out,
                    lhsT=x_codes[:, r, g, here].bitcast(FP8X4),
                    lhsT_scale=x_planes[:, r, g, here],
                    rhs=w_words[:, g, columns].bitcast(FP8X4),
                    rhs_scale=w_planes[4 * g : P, columns],
                    start=(g == 0),
                    stop=(g == PASSES - 1),
                )

        def product_turned(out, r, columns):
            for g in range(PASSES):
                nc.tensor.matmul_mx(
                    out=out,
                    lhsT=w_words[:, g, columns].bitcast(FP8X4),
                    lhsT_scale=w_planes[4 * g : P, columns],
                    rhs=x_codes[:, r, g, :].bitcast(FP8X4),
                    rhs_scale=x_planes[:, r, g, :],
                    start=(g == 0),
                    stop=(g == PASSES - 1),
                )

        def store(result, dst, head0, r, heads=slice(0, TILE_HEADS), slots=slice(0, ROUND_SLOTS)):
            view = dst.rearrange("b h (p j) d -> p (b h) j d", j=SLOTS)
            nc.sync.dma_start(
                out=view[
                    :, head0 + heads.start : head0 + heads.stop, r * ROUND_SLOTS + slots.start : r * ROUND_SLOTS + slots.stop, :
                ],
                in_=result[:, heads, slots, :],
            )

        def value_half(r, s, result):
            bank = psum_brief.tile([P, TILE_HEADS, DH], F32, tag="brief", name="value_bank")
            product(bank[:].rearrange("p h d -> p (h d)"), r, s, slice(V_COL0, V_COL0 + N_TILE))
            nc.scalar.copy(out=result[:, :, s, :], in_=bank[:])
            if s == ROUND_SLOTS - 1:
                store(result, out_2, 0, r)

        tiles = [(out_0, t * TILE_HEADS, t * N_TILE, 0) for t in range(Q_HEADS // TILE_HEADS)]
        tiles.append((out_1, 0, K_COL0, 1))
        order = [(r, t, h) for r in range(GROUPS) for t in range(len(tiles)) for h in range(HALVES)]
        c_banks = {}
        rounds = {}

        def step_matmul(r, t, h):
            state = rounds.setdefault((r, t), {"rstd": {}})
            col0 = tiles[t][2]
            acc = psum_acc.tile([P, N_TILE], F32, tag="acc")
            if t in TURNED:
                pair0 = col0 + h * 2 * DH
                brief = psum_brief.tile([P, ROUND_SLOTS, 2, DH], F32, tag="brief", name="square_bank")
                for s in range(ROUND_SLOTS):
                    product(brief[:, s].rearrange("p h d -> p (h d)"), r, s, slice(pair0, pair0 + 2 * DH))
                state["squared", h] = brief[:].rearrange("p s h d -> p (s h) d")
                for i in range(2):
                    product_turned(acc[:, i * 2 * P : (i + 1) * 2 * P], r, slice(pair0 + i * DH, pair0 + (i + 1) * DH))
            else:
                product(acc[:], r, h, slice(col0, col0 + N_TILE))
                state["squared", h] = acc[:].rearrange("p (h d) -> p h d", d=DH)
            state["acc", h] = acc

        def step_squares(r, t, h):
            state = rounds[r, t]
            squares = work.tile([P, HALF_PAIRS, DH], F32, bufs=2)
            sums = stats.tile([P, HALF_PAIRS], F32)
            for i in range(HALF_PAIRS):
                nc.scalar.activation(
                    out=squares[:, i, :], in_=state["squared", h][:, i, :], func=ACT.Square, accum_out=sums[:, i : i + 1]
                )
            rstd = stats.tile([P, HALF_PAIRS], F32)
            nc.scalar.activation(
                out=rstd[:], in_=sums[:], func=ACT.Abs_reciprocal_sqrt, bias=eps[:, 0:1], scale=1.0 / DH
            )
            state["rstd"][h] = rstd

        def step_multiply(r, t, h):
            state = rounds[r, t]
            acc = state["acc", h]
            if t in TURNED:
                pair = acc[:].rearrange("p (h q) -> p h q", h=2)
                products = work.tile([P, 2, 2, ROUND_SLOTS * P], F32, name="products_turned")
                table = ab_turned[tiles[t][3]][:, :, r * ROUND_SLOTS * P : (r + 1) * ROUND_SLOTS * P]
                nc.vector.tensor_tensor(
                    out=products[:],
                    in0=pair.unsqueeze(1).to_broadcast([P, 2, 2, ROUND_SLOTS * P]),
                    in1=table.unsqueeze(2).to_broadcast([P, 2, 2, ROUND_SLOTS * P]),
                    op=ALU.mult,
                )
                state["products", h] = products
            else:
                if h == 0:
                    products = work.tile([P, 2, ROUND_SLOTS, TILE_HEADS, DH], F32)
                    state["products"] = products
                nc.vector.tensor_tensor(
                    out=state["products"][:, :, h],
                    in0=acc[:].rearrange("p (h d) -> p h d", d=DH).unsqueeze(1).to_broadcast([P, 2, TILE_HEADS, DH]),
                    in1=ab_q[:, r * ROUND_SLOTS + h].unsqueeze(2).to_broadcast([P, 2, TILE_HEADS, DH]),
                    op=ALU.mult,
                )

        def joint_slots(r, t, h):
            if (r, t) == (GROUPS - 1, LAST_UPRIGHT):
                return slice(h, h + 1)
            return slice(0, ROUND_SLOTS) if h == HALVES - 1 else None

        def step_add(r, t, h):
            state = rounds[r, t]
            if t in TURNED:
                if (r, t, h) == order[-1]:
                    bank = psum_acc.tile([P, 2, ROUND_SLOTS, DH], F32, tag="acc", name="last_sum")
                else:
                    bank = psum_sum.tile([P, 2, ROUND_SLOTS, DH], F32, tag="sum")
                products = state["products", h]
                for i in range(2):
                    for s in range(ROUND_SLOTS):
                        for which, permutation in enumerate((identity, exchange)):
                            nc.tensor.matmul(
                                out=bank[:, i, s, :],
                                lhsT=products[:, which, i, s * P : (s + 1) * P],
                                rhs=permutation[:],
                                is_transpose=True,
                                start=(which == 0),
                                stop=(which == 1),
                            )
                state["sum", h] = bank
            else:
                slots = joint_slots(r, t, h)
                if slots is None:
                    return
                if "total" not in state:
                    total = work.tile([P, ROUND_SLOTS, TILE_HEADS, DH], F32)
                    state["total"] = total
                total = state["total"]
                products = state["products"]
                nc.gpsimd.tensor_tensor(
                    out=total[:, slots].rearrange("p s h (a i) -> p (s h) a i", a=2),
                    in0=products[:, 0, slots].rearrange("p s h (a i) -> p (s h) a i", a=2),
                    in1=products[:, 1, slots].rearrange("p s h (a i) -> p (s h) a i", a=2)[:, :, ::-1, :],
                    op=ALU.add,
                )

        def step_finish(r, t, h):
            state = rounds[r, t]
            dst, head0, col0, which = tiles[t]
            if t in TURNED:
                if h == 0:
                    result = results.tile([P, TILE_HEADS, ROUND_SLOTS, DH], F32)
                    state["result"] = result
                result = state["result"]
                heads = slice(2 * h, 2 * h + 2)
                if (r, t, h) == order[-1]:
                    for i in range(2):
                        for s in range(ROUND_SLOTS):
                            j = s * 2 + i
                            nc.vector.scalar_tensor_tensor(
                                out=result[:, 2 * h + i, s, :],
                                in0=state["sum", h][:, i, s, :],
                                scalar=state["rstd"][h][:, j : j + 1],
                                in1=shifts[:, r, s, which, :],
                                op0=ALU.mult,
                                op1=ALU.add,
                            )
                    store(result, dst, head0, r, heads=heads)
                    return
                for i in range(2):
                    for s in range(ROUND_SLOTS):
                        j = s * 2 + i
                        nc.scalar.activation(
                            out=result[:, 2 * h + i, s, :],
                            in_=state["sum", h][:, i, s, :],
                            func=ACT.Copy,
                            scale=state["rstd"][h][:, j : j + 1],
                        )
                very_last = (r, t) == order[-1][:2]
                if very_last or h == HALVES - 1:
                    done = heads if very_last else slice(0, TILE_HEADS)
                    nc.gpsimd.tensor_tensor(
                        out=result[:, done],
                        in0=result[:, done],
                        in1=shifts[:, r, :, which, :]
                        .unsqueeze(1)
                        .to_broadcast([P, done.stop - done.start, ROUND_SLOTS, DH]),
                        op=ALU.add,
                    )
                    store(result, dst, head0, r, heads=done)
            else:
                if "result" not in state:
                    result = results.tile([P, TILE_HEADS, ROUND_SLOTS, DH], F32)
                    state["result"] = result
                result = state["result"]
                for i in range(TILE_HEADS):
                    nc.vector.scalar_tensor_tensor(
                        out=result[:, i, h, :],
                        in0=state["total"][:, h, i, :],
                        scalar=state["rstd"][h][:, i : i + 1],
                        in1=c_banks[r // 2][:, (r % 2) * ROUND_SLOTS + h, :],
                        op0=ALU.mult,
                        op1=ALU.add,
                    )
                slots = joint_slots(r, t, h)
                if slots is not None:
                    store(result, dst, head0, r, slots=slots)

        per_group = len(tiles) * HALVES
        AHEAD = 1
        ADD_LAG = 3
        FINISH_LAG = 8
        LAST_FINISH_LAG = 4
        SHIFT_AT = 2
        TURN_X_AT = 7
        value_steps = {(r + 1) * per_group + s: (r, s) for r in range(GROUPS - 1) for s in range(ROUND_SLOTS)}
        value_steps.update({(GROUPS - 1) * per_group + ROUND_SLOTS + s: (GROUPS - 1, s) for s in range(ROUND_SLOTS)})
        values = {}
        for m in range(-AHEAD, len(order) + FINISH_LAG):
            if m in range(len(order)):
                step_multiply(*order[m])
            if m - ADD_LAG in range(len(order)):
                step_add(*order[m - ADD_LAG])
            if m + AHEAD in range(len(order)):
                step_matmul(*order[m + AHEAD])
            if m - ADD_LAG in range(len(order)) and order[m - ADD_LAG][1] in TURNED:
                step_finish(*order[m - ADD_LAG])
            for lag in (FINISH_LAG, LAST_FINISH_LAG):
                if m - lag in range(len(order)):
                    r, t, h = order[m - lag]
                    very_last = (r, t) == (GROUPS - 1, LAST_UPRIGHT)
                    if t not in TURNED and lag == (LAST_FINISH_LAG if very_last else FINISH_LAG):
                        step_finish(r, t, h)
                        if (r, t, h) == (1, LAST_UPRIGHT, HALVES - 1):
                            c_banks[1] = shift_bank(2)
            if m + AHEAD in range(len(order)):
                step_squares(*order[m + AHEAD])
            if m == SHIFT_AT:
                shift_copy(0)
                c_banks[0] = shift_bank(0)
            if m in value_steps:
                r, s = value_steps[m]
                if s == 0:
                    result = results.tile([P, TILE_HEADS, ROUND_SLOTS, DH], F32)
                    values[r] = result
                value_half(r, s, values[r])
            ahead = m + AHEAD
            if ahead in range(len(order)) and ahead // per_group + 1 < GROUPS:
                r = ahead // per_group + 1
                s = ahead % per_group - TURN_X_AT
                if s in range(ROUND_SLOTS):
                    turn_x(r, s)
                if s == ROUND_SLOTS - 1:
                    quantise_x(r)
                    shift_copy(r)
